import numpy as np
import ml_dtypes


def mxq(x, axis, fmt="e4m3"):
    dtype, down = {"e4m3": (ml_dtypes.float8_e4m3fn, 7), "e5m2": (ml_dtypes.float8_e5m2, 14)}[fmt]
    v = np.moveaxis(np.asarray(x, np.float32).astype(ml_dtypes.bfloat16).astype(np.float64), axis, -1)
    blocks = v.reshape(v.shape[:-1] + (-1, 32))
    amax = np.abs(blocks).max(-1, keepdims=True)
    byte = np.maximum(np.where(amax > 0, np.frexp(amax)[1] - 1 + 127, 0) - down, 1)
    scale = np.exp2(byte - 127.0)
    codes = (blocks / scale).astype(np.float32).astype(dtype).astype(np.float64)
    return np.moveaxis((codes * scale).reshape(v.shape), -1, axis)


WIDE = False


def mx_kscale(k):
    if not WIDE:
        return np.ones(k)
    levels = np.array([10, -10, 5, -5, 0])
    a = np.random.permutation(np.resize(levels, k // 512 * 4)).reshape(k // 512, 4)
    idx = np.arange(k)
    return np.exp2(a[idx // 512, idx % 128 // 32])


BF16 = ml_dtypes.bfloat16


def bf(x):
    return np.asarray(x, np.float32).astype(BF16)


def f64(x):
    return np.asarray(x).astype(np.float64)


E2M1 = np.array([0.0, 0.5, 1.0, 1.5, 2.0, 3.0, 4.0, 6.0, -0.0, -0.5, -1.0, -1.5, -2.0, -3.0, -4.0, -6.0])


def pack_weight(w, fmt):
    k, n = w.shape
    w = f64(bf(w)).reshape(k // 32, 32, n)
    amax = np.abs(w).max(1)
    if fmt == "e4m3":
        byte = np.frexp(amax)[1] - 1 + 127 - 7
    else:
        mant, ex = np.frexp(amax / 6.0)
        byte = np.where(mant > 0.5, ex, ex - 1) + 127
    byte = np.clip(np.where(amax > 0, byte, 1), 1, 254)
    scaled = (w * np.exp2(127.0 - byte)[:, None, :]).reshape(k, n).astype(np.float32)
    by_word = np.ascontiguousarray(scaled.reshape(k // 512, 128, 4, n).transpose(0, 1, 3, 2))
    if fmt == "e4m3":
        words = by_word.astype(ml_dtypes.float8_e4m3fn).view(np.uint8)
    else:
        c = by_word.astype(ml_dtypes.float4_e2m1fn).view(np.uint8) & 0xF
        words = c[..., 0::2] | (c[..., 1::2] << 4)
    return np.ascontiguousarray(words), np.ascontiguousarray(byte.astype(np.uint8).reshape(k // 512, 16, n))


def unpack_weight(words, scales, fmt):
    g, p, n, _ = words.shape
    if fmt == "e4m3":
        vals = np.ascontiguousarray(words).view(ml_dtypes.float8_e4m3fn).astype(np.float64)
    else:
        nib = np.empty((g, p, n, 4), np.uint8)
        nib[..., 0::2] = words & 0xF
        nib[..., 1::2] = words >> 4
        vals = E2M1[nib]
    vals = vals * np.repeat(np.exp2(scales.astype(np.float64) - 127.0), 8, axis=1)[..., None]
    return vals.transpose(0, 1, 3, 2).reshape(g * 512, n)

def pack4(w):
    words, scales = pack_weight(w, "e2m1")
    return words.reshape(words.shape[0], 128, -1), scales


def unpack4(words, scales):
    return unpack_weight(words.reshape(words.shape[0], 128, -1, 2), scales, "e2m1")


B, IN, H = 2048, 512, 512
G = 4 * H
EPS = 1e-5


def _layernorm(v, gamma, beta):
    mean = np.mean(v, axis=-1, keepdims=True)
    var = np.mean(np.square(v - mean), axis=-1, keepdims=True)
    return (v - mean) / np.sqrt(var + EPS) * gamma + beta


def sigmoid(v):
    return 1.0 / (1.0 + np.exp(-v))


def setup_inputs():
    s, t = mx_kscale(IN), mx_kscale(H)
    x = bf(np.random.standard_normal((B, IN)) * s)
    h_prev = bf(np.random.standard_normal((B, H)) * t)
    c_prev = bf(np.random.standard_normal((B, H)))
    W_ih_words, W_ih_scales = pack4(np.random.standard_normal((IN, G)) / np.sqrt(IN) / s[:, None])
    W_hh_words, W_hh_scales = pack4(np.random.standard_normal((H, G)) / np.sqrt(H) / t[:, None])
    return {
        "x": x,
        "h_prev": h_prev,
        "c_prev": c_prev,
        "W_ih_words": W_ih_words,
        "W_ih_scales": W_ih_scales,
        "W_hh_words": W_hh_words,
        "W_hh_scales": W_hh_scales,
        "gamma_ih": bf(1.0 + 0.2 * np.random.standard_normal(G)),
        "beta_ih": bf(0.3 * np.random.standard_normal(G)),
        "gamma_hh": bf(1.0 + 0.2 * np.random.standard_normal(G)),
        "beta_hh": bf(0.3 * np.random.standard_normal(G)),
        "gamma_c": bf(1.0 + 0.2 * np.random.standard_normal(H)),
        "beta_c": bf(0.3 * np.random.standard_normal(H)),
    }


def reference(x, h_prev, c_prev, W_ih_words, W_ih_scales, W_hh_words, W_hh_scales, gamma_ih, beta_ih, gamma_hh, beta_hh, gamma_c, beta_c):
    a_ih = mxq(f64(x), 1, "e4m3") @ unpack4(W_ih_words, W_ih_scales)
    a_hh = mxq(f64(h_prev), 1, "e4m3") @ unpack4(W_hh_words, W_hh_scales)
    gates_ih = _layernorm(a_ih, f64(gamma_ih), f64(beta_ih))
    gates_hh = _layernorm(a_hh, f64(gamma_hh), f64(beta_hh))
    gates = gates_ih + gates_hh
    i_g, f_g, g_g, o_g = np.split(gates, 4, axis=1)
    i_t = sigmoid(i_g)
    f_t = sigmoid(f_g)
    g_t = np.tanh(g_g)
    o_t = sigmoid(o_g)
    c_t = f_t * f64(c_prev) + i_t * g_t
    h_t = o_t * np.tanh(_layernorm(c_t, f64(gamma_c), f64(beta_c)))
    return (h_t, c_t)

@@ -1,0 +1,415 @@
+from contextlib import ExitStack
+
+import concourse.masks as masks
+import concourse.mybir as mybir
+
+F32 = mybir.dt.float32
+BF16 = mybir.dt.bfloat16
+I32 = mybir.dt.int32
+U32 = mybir.dt.uint32
+U8 = mybir.dt.uint8
+FP8X4 = mybir.dt.float8_e4m3fn_x4
+FP4X4 = mybir.dt.float4_e2m1fn_x4
+ALU = mybir.AluOpType
+ACT = mybir.ActivationFunctionType
+
+P = 128
+BATCH = 2048
+K = 512
+GATES = 2048
+HID = 512
+BANK = 512
+HALF = 2 * BANK
+TILES = BATCH // P
+EPS = 1e-5
+
+FLOPS = 2 * 2 * BATCH * K * GATES
+
+
+def tile_layernormlstmcell_kernel(
+    tc,
+    x,
+    h_prev,
+    c_prev,
+    W_ih_words,
+    W_ih_scales,
+    W_hh_words,
+    W_hh_scales,
+    gamma_ih,
+    beta_ih,
+    gamma_hh,
+    beta_hh,
+    gamma_c,
+    beta_c,
+    out_0,
+    out_1,
+):
+    nc = tc.nc
+    with ExitStack() as ctx:
+        ctx.enter_context(tc.manual_schedule())
+        keep = ctx.enter_context(tc.tile_pool(name="keep", bufs=1))
+        work2 = ctx.enter_context(tc.tile_pool(name="work2", bufs=2))
+        work3 = ctx.enter_context(tc.tile_pool(name="work3", bufs=3))
+        ps_norm = ctx.enter_context(tc.psum_pool(name="ps_norm", bufs=4))
+        ps_var = ctx.enter_context(tc.psum_pool(name="ps_var", bufs=2))
+        ps_sum = ctx.enter_context(tc.psum_pool(name="ps_sum", bufs=1))
+        ps_turn = ctx.enter_context(tc.psum_pool(name="ps_turn", bufs=1))
+
+        rows_sb = [
+            keep.tile([P, TILES, K], BF16, name="x_sb"),
+            keep.tile([P, TILES, K], BF16, name="h_sb"),
+        ]
+        c_sb = keep.tile([P, TILES, HID], BF16)
+        w_words = [
+            keep.tile([P, 2 * GATES], U8, name="w_ih_words", align_bytes=64),
+            keep.tile([P, 2 * GATES], U8, name="w_hh_words", align_bytes=64),
+        ]
+        w_scales = [
+            keep.tile([P, GATES], U8, name="w_ih_plane", align_bytes=64),
+            keep.tile([P, GATES], U8, name="w_hh_plane", align_bytes=64),
+        ]
+        a_words = keep.tile([P, TILES, 2 * P], U32, align_bytes=64)
+        a_scales = keep.tile([P, TILES, 2 * P], U8, align_bytes=64)
+        gain = [
+            keep.tile([P, GATES], BF16, name="gain_ih"),
+            keep.tile([P, GATES], BF16, name="gain_hh"),
+        ]
+        shift_ih = keep.tile([P, GATES], BF16)
+        shift_hh = keep.tile([P, GATES], BF16)
+        shift = keep.tile([P, GATES], F32)
+        gain_c = keep.tile([P, HID], BF16)
+        shift_c = keep.tile([P, HID], BF16)
+        ident = keep.tile([P, P], F32)
+        neg_half = keep.tile([P, 2], F32)
+        warm = keep.tile([P, 1], F32)
+
+        for plane in w_scales:
+            nc.vector.memset(plane[:].bitcast(I32), 0)
+        nc.vector.memset(neg_half[:], -0.5)
+        masks.make_identity(nc, ident[:])
+        nc.scalar.activation(out=warm[:], in_=neg_half[:, 0:1], func=ACT.Sigmoid)
+
+        rows_dram = [
+            x.rearrange("(p t) k -> p t k", t=TILES),
+            h_prev.rearrange("(p t) k -> p t k", t=TILES),
+        ]
+        c_dram = c_prev.rearrange("(p t) n -> p t n", t=TILES)
+        h_out = out_0.rearrange("(p t) n -> p t n", t=TILES)
+        c_out = out_1.rearrange("(p t) n -> p t n", t=TILES)
+
+        def load_rows(first, last):
+            for o in range(2):
+                nc.sync.dma_start(out=rows_sb[o][:, first:last, :], in_=rows_dram[o][:, first:last, :])
+
+        load_rows(0, 2)
+        for o, scales in enumerate((W_ih_scales, W_hh_scales)):
+            for quad in range(4):
+                nc.sync.dma_start(
+                    out=w_scales[o][32 * quad : 32 * quad + 4, :].bitcast(I32),
+                    in_=scales[0, 4 * quad : 4 * quad + 4, :].bitcast(I32),
+                )
+        for o, words in enumerate((W_ih_words, W_hh_words)):
+            nc.sync.dma_start(out=w_words[o][:].bitcast(I32), in_=words[0].bitcast(I32))
+        load_rows(2, 8)
+        nc.sync.dma_start(out=c_sb[:, 0:8, :], in_=c_dram[:, 0:8, :])
+        load_rows(8, TILES)
+        nc.sync.dma_start(out=c_sb[:, 8:TILES, :], in_=c_dram[:, 8:TILES, :])
+        nc.scalar.dma_start(out=gain[0][:], in_=gamma_ih.partition_broadcast(P))
+        nc.scalar.dma_start(out=gain[1][:], in_=gamma_hh.partition_broadcast(P))
+        nc.scalar.dma_start(out=shift_ih[:], in_=beta_ih.partition_broadcast(P))
+        nc.scalar.dma_start(out=shift_hh[:], in_=beta_hh.partition_broadcast(P))
+        nc.scalar.dma_start(out=gain_c[:], in_=gamma_c.partition_broadcast(P))
+        nc.scalar.dma_start(out=shift_c[:], in_=beta_c.partition_broadcast(P))
+        nc.gpsimd.tensor_tensor(out=shift[:], in0=shift_ih[:], in1=shift_hh[:], op=ALU.add)
+
+        grouped = {}
+        neg_mean = {}
+        sq_sums = {}
+        rstd = {}
+        products = {}
+        centred = {}
+        act_if = {}
+        act_g = {}
+        act_o = {}
+        keep_part = {}
+        new_part = {}
+        cell = {}
+        cell_sum = {}
+        cell_neg_mean = {}
+        cell_rstd = {}
+        cell_norm = {}
+        cell_tanh = {}
+
+        def mx_pass(out, t, o, first_col, n_cols, start, stop):
+            nc.tensor.matmul_mx(
+                out=out,
+                lhsT=a_words[:, t, o * P : (o + 1) * P].bitcast(FP8X4),
+                lhsT_scale=a_scales[:, t, o * P : (o + 1) * P],
+                rhs=w_words[o][:, 2 * first_col : 2 * (first_col + n_cols)].bitcast(FP4X4),
+                rhs_scale=w_scales[o][:, first_col : first_col + n_cols],
+                start=start,
+                stop=stop,
+            )
+
+        def turn(t):
+            turned = ps_turn.tile([P, 4, P], F32)
+            for o in range(2):
+                words = rows_sb[o][:, t, :].bitcast(F32)
+                for u in range(2):
+                    nc.tensor.transpose(turned[:, 2 * o + u, :], words[:, u : K // 2 : 2], ident[:])
+            grouped[t] = work2.tile([P, 2 * P * 4], BF16, name="grouped", align_bytes=64)
+            nc.scalar.copy(
+                out=grouped[t][:].bitcast(F32).rearrange("p (o b u) -> p o b u", o=2, u=2),
+                in_=turned[:].rearrange("p (o u) b -> p o b u", u=2),
+            )
+
+        def quantise(t):
+            nc.vector.quantize_mx(
+                out=a_words[:, t, :].bitcast(FP8X4), scales=a_scales[:, t, :], in_=grouped[t][:]
+            )
+
+        def mean_passes(t):
+            blocks = GATES // P
+            sums = ps_sum.tile([P, 2, P], F32)
+            for o in range(2):
+                for c in range(blocks):
+                    mx_pass(sums[:, o, :], t, o, c * P, P, c == 0, c == blocks - 1)
+            return sums
+
+        def mean(t, sums):
+            neg_mean[t] = work3.tile([P, 2], F32, name="neg_mean")
+            for o in range(2):
+                scrap = work2.tile([P, P], F32, name="scrap_mean")
+                nc.scalar.activation(
+                    out=scrap[:],
+                    in_=sums[:, o, :],
+                    func=ACT.Copy,
+                    scale=-1.0 / GATES,
+                    accum_out=neg_mean[t][:, o : o + 1],
+                )
+            sq_sums[t] = work3.tile([P, 2, 4], F32, name="sq_sums")
+
+        def var_pass(t, bank):
+            o, j = divmod(bank, 4)
+            product = ps_var.tile([P, BANK], F32, name="var_product")
+            mx_pass(product[:], t, o, j * BANK, BANK, True, True)
+            return product
+
+        def var_square(t, bank, product):
+            o, j = divmod(bank, 4)
+            scrap = work2.tile([P, BANK], F32, name="scrap_square")
+            nc.scalar.activation(
+                out=scrap[:],
+                in_=product[:],
+                func=ACT.Square,
+                bias=neg_mean[t][:, o : o + 1],
+                scale=1.0,
+                accum_out=sq_sums[t][:, o, j : j + 1],
+            )
+
+        def inverse_std(total, n, name):
+            width = total.shape[1]
+            var_eps = work3.tile([P, width], F32, name=name + "_var")
+            nc.gpsimd.tensor_scalar(
+                out=var_eps[:], in0=total[:], scalar1=1.0 / n, scalar2=EPS, op0=ALU.mult, op1=ALU.add
+            )
+            result = work3.tile([P, width], F32, name=name)
+            nc.gpsimd.tensor_tensor(out=result[:], in0=var_eps[:], in1=neg_half[:, 0:width], op=ALU.pow)
+            return result
+
+        def gate_rstd(t):
+            total = work3.tile([P, 2], F32, name="sq_total")
+            for o in range(2):
+                scrap = work2.tile([P, 4], F32, name="scrap_total")
+                nc.scalar.activation(
+                    out=scrap[:], in_=sq_sums[t][:, o, :], func=ACT.Copy, accum_out=total[:, o : o + 1]
+                )
+            rstd[t] = inverse_std(total, GATES, "rstd")
+
+        def norm_passes(t, half):
+            products[t, half] = []
+            for j in (2 * half, 2 * half + 1):
+                for o in range(2):
+                    product = ps_norm.tile([P, BANK], F32, name="norm_product")
+                    mx_pass(product[:], t, o, j * BANK, BANK, True, True)
+                    products[t, half].append((j, o, product))
+
+        def centre_and_gain(t, half):
+            centred[t, half] = [
+                work2.tile([P, HALF], F32, name="centred_ih"),
+                work2.tile([P, HALF], F32, name="centred_hh"),
+            ]
+            for j, o, product in products[t, half]:
+                nc.vector.scalar_tensor_tensor(
+                    out=centred[t, half][o][:, (j % 2) * BANK : (j % 2 + 1) * BANK],
+                    in0=product[:],
+                    scalar=neg_mean[t][:, o : o + 1],
+                    in1=gain[o][:, j * BANK : (j + 1) * BANK],
+                    op0=ALU.add,
+                    op1=ALU.mult,
+                )
+
+        def scale_and_shift(t, half):
+            part = centred[t, half][0]
+            nc.vector.scalar_tensor_tensor(
+                out=part[:],
+                in0=part[:],
+                scalar=rstd[t][:, 0:1],
+                in1=shift[:, half * HALF : (half + 1) * HALF],
+                op0=ALU.mult,
+                op1=ALU.add,
+            )
+
+        def scale_and_add(t, half):
+            part = centred[t, half][1]
+            nc.vector.scalar_tensor_tensor(
+                out=part[:],
+                in0=part[:],
+                scalar=rstd[t][:, 1:2],
+                in1=centred[t, half][0][:],
+                op0=ALU.mult,
+                op1=ALU.add,
+            )
+
+        def squash_if(t):
+            act_if[t] = work2.tile([P, HALF], F32, name="act_if")
+            nc.scalar.activation(out=act_if[t][:], in_=centred[t, 0][1][:], func=ACT.Sigmoid)
+
+        def squash_go(t):
+            act_g[t] = work2.tile([P, HID], F32, name="act_g")
+            act_o[t] = work3.tile([P, HID], F32, name="act_o")
+            nc.scalar.activation(out=act_g[t][:], in_=centred[t, 1][1][:, 0:HID], func=ACT.Tanh)
+            nc.scalar.activation(out=act_o[t][:], in_=centred[t, 1][1][:, HID:HALF], func=ACT.Sigmoid)
+
+        def keep_old(t):
+            keep_part[t] = work2.tile([P, HID], F32, name="keep_part")
+            nc.vector.tensor_tensor(
+                out=keep_part[t][:], in0=act_if[t][:, HID:HALF], in1=c_sb[:, t, :], op=ALU.mult
+            )
+
+        def take_new(t):
+            new_part[t] = work2.tile([P, HID], F32, name="new_part")
+            nc.vector.tensor_tensor(
+                out=new_part[t][:], in0=act_if[t][:, 0:HID], in1=act_g[t][:], op=ALU.mult
+            )
+
+        def new_cell(t):
+            cell[t] = work3.tile([P, HID], F32, name="cell")
+            cell_sum[t] = work3.tile([P, 1], F32, name="cell_sum")
+            nc.vector.scalar_tensor_tensor(
+                out=cell[t][:],
+                in0=keep_part[t][:],
+                scalar=1.0,
+                in1=new_part[t][:],
+                op0=ALU.mult,
+                op1=ALU.add,
+                accum_out=cell_sum[t][:],
+            )
+            nc.sync.dma_start(out=c_out[:, t, :], in_=cell[t][:])
+
+        def cell_stats(t):
+            cell_neg_mean[t] = work3.tile([P, 1], F32, name="cell_neg_mean")
+            nc.scalar.mul(out=cell_neg_mean[t][:], in_=cell_sum[t][:], mul=-1.0 / HID)
+            scrap = work2.tile([P, BANK], F32, name="scrap_square")
+            total = work3.tile([P, 1], F32, name="cell_sq_total")
+            nc.scalar.activation(
+                out=scrap[:],
+                in_=cell[t][:],
+                func=ACT.Square,
+                bias=cell_neg_mean[t][:],
+                scale=1.0,
+                accum_out=total[:],
+            )
+            cell_rstd[t] = inverse_std(total, HID, "cell_rstd")
+
+        def cell_centre_and_gain(t):
+            cell_norm[t] = work3.tile([P, HID], F32, name="cell_norm")
+            nc.vector.scalar_tensor_tensor(
+                out=cell_norm[t][:],
+                in0=cell[t][:],
+                scalar=cell_neg_mean[t][:],
+                in1=gain_c[:],
+                op0=ALU.add,
+                op1=ALU.mult,
+            )
+
+        def cell_scale_and_shift(t):
+            nc.vector.scalar_tensor_tensor(
+                out=cell_norm[t][:],
+                in0=cell_norm[t][:],
+                scalar=cell_rstd[t][:],
+                in1=shift_c[:],
+                op0=ALU.mult,
+                op1=ALU.add,
+            )
+
+        def squash_cell(t):
+            cell_tanh[t] = work2.tile([P, HID], F32, name="cell_tanh")
+            nc.scalar.activation(out=cell_tanh[t][:], in_=cell_norm[t][:], func=ACT.Tanh)
+
+        def hidden(t):
+            h_new = work3.tile([P, HID], F32, name="h_new")
+            nc.vector.tensor_tensor(out=h_new[:], in0=act_o[t][:], in1=cell_tanh[t][:], op=ALU.mult)
+            nc.sync.dma_start(out=h_out[:, t, :], in_=h_new[:])
+
+        def live(t):
+            return 0 <= t < TILES
+
+        for t in range(-3, TILES + 2):
+            if live(t):
+                centre_and_gain(t, 0)
+            if live(t - 1):
+                squash_go(t - 1)
+            if live(t - 2):
+                squash_cell(t - 2)
+            var_products = {}
+            if live(t + 1):
+                sums = mean_passes(t + 1)
+                var_products[0] = var_pass(t + 1, 0)
+                var_products[1] = var_pass(t + 1, 1)
+            if live(t):
+                norm_passes(t, 1)
+
+            if live(t - 1):
+                take_new(t - 1)
+            if live(t - 2):
+                hidden(t - 2)
+            if live(t):
+                scale_and_shift(t, 0)
+            if live(t - 1):
+                new_cell(t - 1)
+            if live(t):
+                scale_and_add(t, 0)
+            if live(t + 1):
+                mean(t + 1, sums)
+                for bank in range(5):
+                    var_square(t + 1, bank, var_products[bank])
+                    var_products[bank + 2] = var_pass(t + 1, bank + 2)
+
+            if live(t):
+                centre_and_gain(t, 1)
+            if live(t + 1):
+                norm_passes(t + 1, 0)
+            if live(t - 1):
+                cell_stats(t - 1)
+            if live(t):
+                squash_if(t)
+
+            if live(t - 1):
+                cell_centre_and_gain(t - 1)
+            if live(t):
+                scale_and_shift(t, 1)
+                keep_old(t)
+                scale_and_add(t, 1)
+            if live(t - 1):
+                cell_scale_and_shift(t - 1)
+            if live(t + 2):
+                quantise(t + 2)
+            if live(t + 1):
+                var_square(t + 1, 5, var_products[5])
+                var_products[7] = var_pass(t + 1, 7)
+                var_square(t + 1, 6, var_products[6])
+                var_square(t + 1, 7, var_products[7])
+                gate_rstd(t + 1)
+            if live(t + 3):
+                turn(t + 3)

@@ -20,6 +20,9 @@ GATES = 2048
 HID = 512
 BANK = 512
 HALF = 2 * BANK
+PRODUCT_BANKS = GATES // BANK
+BANKS = 2 * PRODUCT_BANKS
+AHEAD = 6
 TILES = BATCH // P
 EPS = 1e-5
 
@@ -50,8 +53,8 @@ def tile_layernormlstmcell_kernel(
         keep = ctx.enter_context(tc.tile_pool(name="keep", bufs=1))
         work2 = ctx.enter_context(tc.tile_pool(name="work2", bufs=2))
         work3 = ctx.enter_context(tc.tile_pool(name="work3", bufs=3))
-        ps_norm = ctx.enter_context(tc.psum_pool(name="ps_norm", bufs=4))
-        ps_var = ctx.enter_context(tc.psum_pool(name="ps_var", bufs=2))
+        work4 = ctx.enter_context(tc.tile_pool(name="work4", bufs=4))
+        ps_prod = ctx.enter_context(tc.psum_pool(name="ps_prod", bufs=AHEAD))
         ps_sum = ctx.enter_context(tc.psum_pool(name="ps_sum", bufs=1))
         ps_turn = ctx.enter_context(tc.psum_pool(name="ps_turn", bufs=1))
 
@@ -80,14 +83,14 @@ def tile_layernormlstmcell_kernel(
         gain_c = keep.tile([P, HID], BF16)
         shift_c = keep.tile([P, HID], BF16)
         ident = keep.tile([P, P], F32)
-        neg_half = keep.tile([P, 2], F32)
+        neg_half = keep.tile([P, 1], F32)
         warm = keep.tile([P, 1], F32)
 
         for plane in w_scales:
             nc.vector.memset(plane[:].bitcast(I32), 0)
         nc.vector.memset(neg_half[:], -0.5)
         masks.make_identity(nc, ident[:])
-        nc.scalar.activation(out=warm[:], in_=neg_half[:, 0:1], func=ACT.Sigmoid)
+        nc.scalar.activation(out=warm[:], in_=neg_half[:], func=ACT.Sigmoid)
 
         rows_dram = [
             x.rearrange("(p t) k -> p t k", t=TILES),
@@ -110,7 +113,8 @@ def tile_layernormlstmcell_kernel(
                 )
         for o, words in enumerate((W_ih_words, W_hh_words)):
             nc.sync.dma_start(out=w_words[o][:].bitcast(I32), in_=words[0].bitcast(I32))
-        load_rows(2, 8)
+        load_rows(2, 4)
+        load_rows(4, 8)
         nc.sync.dma_start(out=c_sb[:, 0:8, :], in_=c_dram[:, 0:8, :])
         load_rows(8, TILES)
         nc.sync.dma_start(out=c_sb[:, 8:TILES, :], in_=c_dram[:, 8:TILES, :])
@@ -187,20 +191,19 @@ def tile_layernormlstmcell_kernel(
                     scale=-1.0 / GATES,
                     accum_out=neg_mean[t][:, o : o + 1],
                 )
-            sq_sums[t] = work3.tile([P, 2, 4], F32, name="sq_sums")
+            sq_sums[t] = work3.tile([P, 2, PRODUCT_BANKS], F32, name="sq_sums")
 
-        def var_pass(t, bank):
-            o, j = divmod(bank, 4)
-            product = ps_var.tile([P, BANK], F32, name="var_product")
-            mx_pass(product[:], t, o, j * BANK, BANK, True, True)
-            return product
+        def product_pass(t, bank):
+            o, j = divmod(bank, PRODUCT_BANKS)
+            products[t, bank] = ps_prod.tile([P, BANK], F32, name="product")
+            mx_pass(products[t, bank][:], t, o, j * BANK, BANK, True, True)
 
-        def var_square(t, bank, product):
-            o, j = divmod(bank, 4)
+        def square(t, bank):
+            o, j = divmod(bank, PRODUCT_BANKS)
             scrap = work2.tile([P, BANK], F32, name="scrap_square")
             nc.scalar.activation(
                 out=scrap[:],
-                in_=product[:],
+                in_=products[t, bank][:],
                 func=ACT.Square,
                 bias=neg_mean[t][:, o : o + 1],
                 scale=1.0,
@@ -208,78 +211,69 @@ def tile_layernormlstmcell_kernel(
             )
 
         def inverse_std(total, n, name):
-            width = total.shape[1]
-            var_eps = work3.tile([P, width], F32, name=name + "_var")
+            var_eps = work4.tile([P, 1], F32, name=name + "_var")
             nc.gpsimd.tensor_scalar(
                 out=var_eps[:], in0=total[:], scalar1=1.0 / n, scalar2=EPS, op0=ALU.mult, op1=ALU.add
             )
-            result = work3.tile([P, width], F32, name=name)
-            nc.gpsimd.tensor_tensor(out=result[:], in0=var_eps[:], in1=neg_half[:, 0:width], op=ALU.pow)
+            result = work4.tile([P, 1], F32, name=name)
+            nc.gpsimd.tensor_tensor(out=result[:], in0=var_eps[:], in1=neg_half[:], op=ALU.pow)
             return result
 
-        def gate_rstd(t):
-            total = work3.tile([P, 2], F32, name="sq_total")
-            for o in range(2):
-                scrap = work2.tile([P, 4], F32, name="scrap_total")
-                nc.scalar.activation(
-                    out=scrap[:], in_=sq_sums[t][:, o, :], func=ACT.Copy, accum_out=total[:, o : o + 1]
-                )
-            rstd[t] = inverse_std(total, GATES, "rstd")
+        def gate_rstd(t, o):
+            total = work4.tile([P, 1], F32, name="sq_total")
+            scrap = work2.tile([P, PRODUCT_BANKS], F32, name="scrap_total")
+            nc.scalar.activation(out=scrap[:], in_=sq_sums[t][:, o, :], func=ACT.Copy, accum_out=total[:])
+            rstd[t, o] = inverse_std(total, GATES, "rstd")
 
-        def norm_passes(t, half):
-            products[t, half] = []
-            for j in (2 * half, 2 * half + 1):
-                for o in range(2):
-                    product = ps_norm.tile([P, BANK], F32, name="norm_product")
-                    mx_pass(product[:], t, o, j * BANK, BANK, True, True)
-                    products[t, half].append((j, o, product))
-
-        def centre_and_gain(t, half):
-            centred[t, half] = [
-                work2.tile([P, HALF], F32, name="centred_ih"),
-                work2.tile([P, HALF], F32, name="centred_hh"),
-            ]
-            for j, o, product in products[t, half]:
-                nc.vector.scalar_tensor_tensor(
-                    out=centred[t, half][o][:, (j % 2) * BANK : (j % 2 + 1) * BANK],
-                    in0=product[:],
-                    scalar=neg_mean[t][:, o : o + 1],
-                    in1=gain[o][:, j * BANK : (j + 1) * BANK],
-                    op0=ALU.add,
-                    op1=ALU.mult,
-                )
+        def centre_and_gain(t, bank):
+            o, j = divmod(bank, PRODUCT_BANKS)
+            if bank == 0:
+                centred[t] = [
+                    work2.tile([P, GATES], F32, name="centred_ih"),
+                    work2.tile([P, GATES], F32, name="centred_hh"),
+                ]
+            nc.vector.scalar_tensor_tensor(
+                out=centred[t][o][:, j * BANK : (j + 1) * BANK],
+                in0=products[t, bank][:],
+                scalar=neg_mean[t][:, o : o + 1],
+                in1=gain[o][:, j * BANK : (j + 1) * BANK],
+                op0=ALU.add,
+                op1=ALU.mult,
+            )
 
         def scale_and_shift(t, half):
-            part = centred[t, half][0]
+            cols = slice(half * HALF, (half + 1) * HALF)
             nc.vector.scalar_tensor_tensor(
-                out=part[:],
-                in0=part[:],
-                scalar=rstd[t][:, 0:1],
-                in1=shift[:, half * HALF : (half + 1) * HALF],
+                out=centred[t][0][:, cols],
+                in0=centred[t][0][:, cols],
+                scalar=rstd[t, 0][:],
+                in1=shift[:, cols],
                 op0=ALU.mult,
                 op1=ALU.add,
             )
 
         def scale_and_add(t, half):
-            part = centred[t, half][1]
+            cols = slice(half * HALF, (half + 1) * HALF)
             nc.vector.scalar_tensor_tensor(
-                out=part[:],
-                in0=part[:],
-                scalar=rstd[t][:, 1:2],
-                in1=centred[t, half][0][:],
+                out=centred[t][1][:, cols],
+                in0=centred[t][1][:, cols],
+                scalar=rstd[t, 1][:],
+                in1=centred[t][0][:, cols],
                 op0=ALU.mult,
                 op1=ALU.add,
             )
 
         def squash_if(t):
             act_if[t] = work2.tile([P, HALF], F32, name="act_if")
-            nc.scalar.activation(out=act_if[t][:], in_=centred[t, 0][1][:], func=ACT.Sigmoid)
+            nc.scalar.activation(out=act_if[t][:], in_=centred[t][1][:, 0:HALF], func=ACT.Sigmoid)
 
-        def squash_go(t):
+        def squash_g(t):
             act_g[t] = work2.tile([P, HID], F32, name="act_g")
+            nc.scalar.activation(out=act_g[t][:], in_=centred[t][1][:, HALF : HALF + HID], func=ACT.Tanh)
+
+        def squash_o(t):
             act_o[t] = work3.tile([P, HID], F32, name="act_o")
-            nc.scalar.activation(out=act_g[t][:], in_=centred[t, 1][1][:, 0:HID], func=ACT.Tanh)
-            nc.scalar.activation(out=act_o[t][:], in_=centred[t, 1][1][:, HID:HALF], func=ACT.Sigmoid)
+            nc.scalar.activation(out=act_o[t][:], in_=centred[t][1][:, HALF + HID : GATES], func=ACT.Sigmoid)
 
         def keep_old(t):
             keep_part[t] = work2.tile([P, HID], F32, name="keep_part")
@@ -355,61 +349,43 @@ def tile_layernormlstmcell_kernel(
         def live(t):
             return 0 <= t < TILES
 
-        for t in range(-3, TILES + 2):
-            if live(t):
-                centre_and_gain(t, 0)
-            if live(t - 1):
-                squash_go(t - 1)
-            if live(t - 2):
-                squash_cell(t - 2)
-            var_products = {}
-            if live(t + 1):
-                sums = mean_passes(t + 1)
-                var_products[0] = var_pass(t + 1, 0)
-                var_products[1] = var_pass(t + 1, 1)
-            if live(t):
-                norm_passes(t, 1)
-
-            if live(t - 1):
-                take_new(t - 1)
-            if live(t - 2):
-                hidden(t - 2)
-            if live(t):
-                scale_and_shift(t, 0)
-            if live(t - 1):
-                new_cell(t - 1)
-            if live(t):
-                scale_and_add(t, 0)
-            if live(t + 1):
-                mean(t + 1, sums)
-                for bank in range(5):
-                    var_square(t + 1, bank, var_products[bank])
-                    var_products[bank + 2] = var_pass(t + 1, bank + 2)
-
-            if live(t):
-                centre_and_gain(t, 1)
-            if live(t + 1):
-                norm_passes(t + 1, 0)
+        for t in range(-4, TILES + 1):
             if live(t - 1):
                 cell_stats(t - 1)
-            if live(t):
-                squash_if(t)
+            for bank in range(BANKS):
+                if live(t):
+                    centre_and_gain(t, bank)
+                later_t, later_bank = t + (bank + AHEAD) // BANKS, (bank + AHEAD) % BANKS
+                if live(later_t):
+                    product_pass(later_t, later_bank)
+                    square(later_t, later_bank)
+                    if later_bank % PRODUCT_BANKS == PRODUCT_BANKS - 1:
+                        gate_rstd(later_t, later_bank // PRODUCT_BANKS)
 
+            if live(t + 2):
+                mean(t + 2, mean_passes(t + 2))
+            if live(t + 4):
+                turn(t + 4)
+            if live(t):
+                scale_and_shift(t, 0)
+                scale_and_shift(t, 1)
             if live(t - 1):
                 cell_centre_and_gain(t - 1)
             if live(t):
-                scale_and_shift(t, 1)
-                keep_old(t)
+                scale_and_add(t, 0)
+                squash_if(t)
                 scale_and_add(t, 1)
+                squash_g(t)
             if live(t - 1):
                 cell_scale_and_shift(t - 1)
-            if live(t + 2):
-                quantise(t + 2)
-            if live(t + 1):
-                var_square(t + 1, 5, var_products[5])
-                var_products[7] = var_pass(t + 1, 7)
-                var_square(t + 1, 6, var_products[6])
-                var_square(t + 1, 7, var_products[7])
-                gate_rstd(t + 1)
+                squash_cell(t - 1)
+            if live(t):
+                squash_o(t)
+                keep_old(t)
+                take_new(t)
+            if live(t - 1):
+                hidden(t - 1)
+            if live(t):
+                new_cell(t)
             if live(t + 3):
-                turn(t + 3)
+                quantise(t + 3)

@@ -100,30 +100,33 @@ def tile_layernormlstmcell_kernel(
         h_out = out_0.rearrange("(p t) n -> p t n", t=TILES)
         c_out = out_1.rearrange("(p t) n -> p t n", t=TILES)
 
-        def load_rows(first, last):
-            for o in range(2):
-                nc.sync.dma_start(out=rows_sb[o][:, first:last, :], in_=rows_dram[o][:, first:last, :])
-
-        load_rows(0, 2)
-        for o, scales in enumerate((W_ih_scales, W_hh_scales)):
+        def load_scales(o, scales):
             for quad in range(4):
                 nc.sync.dma_start(
                     out=w_scales[o][32 * quad : 32 * quad + 4, :].bitcast(I32),
                     in_=scales[0, 4 * quad : 4 * quad + 4, :].bitcast(I32),
                 )
-        for o, words in enumerate((W_ih_words, W_hh_words)):
-            nc.sync.dma_start(out=w_words[o][:].bitcast(I32), in_=words[0].bitcast(I32))
-        load_rows(2, 4)
-        load_rows(4, 8)
-        nc.sync.dma_start(out=c_sb[:, 0:8, :], in_=c_dram[:, 0:8, :])
-        load_rows(8, TILES)
-        nc.sync.dma_start(out=c_sb[:, 8:TILES, :], in_=c_dram[:, 8:TILES, :])
-        nc.scalar.dma_start(out=gain[0][:], in_=gamma_ih.partition_broadcast(P))
-        nc.scalar.dma_start(out=gain[1][:], in_=gamma_hh.partition_broadcast(P))
-        nc.scalar.dma_start(out=shift_ih[:], in_=beta_ih.partition_broadcast(P))
-        nc.scalar.dma_start(out=shift_hh[:], in_=beta_hh.partition_broadcast(P))
-        nc.scalar.dma_start(out=gain_c[:], in_=gamma_c.partition_broadcast(P))
-        nc.scalar.dma_start(out=shift_c[:], in_=beta_c.partition_broadcast(P))
+
+        def load_rows(o, first, last):
+            nc.sync.dma_start(out=rows_sb[o][:, first:last, :], in_=rows_dram[o][:, first:last, :])
+
+        load_scales(0, W_ih_scales)
+        load_rows(0, 0, 2)
+        nc.sync.dma_start(out=w_words[0][:].bitcast(I32), in_=W_ih_words[0].bitcast(I32))
+        load_rows(1, 0, 2)
+        nc.sync.dma_start(out=w_words[1][:].bitcast(I32), in_=W_hh_words[0].bitcast(I32))
+        load_scales(1, W_hh_scales)
+        for first, last in ((2, 4), (4, 8), (8, TILES)):
+            load_rows(0, first, last)
+            load_rows(1, first, last)
+            nc.sync.dma_start(out=c_sb[:, first - 2 : last - 2, :], in_=c_dram[:, first - 2 : last - 2, :])
+        nc.sync.dma_start(out=c_sb[:, TILES - 2 : TILES, :], in_=c_dram[:, TILES - 2 : TILES, :])
+        nc.gpsimd.dma_start(out=gain[0][:], in_=gamma_ih.partition_broadcast(P))
+        nc.gpsimd.dma_start(out=gain[1][:], in_=gamma_hh.partition_broadcast(P))
+        nc.gpsimd.dma_start(out=shift_ih[:], in_=beta_ih.partition_broadcast(P))
+        nc.gpsimd.dma_start(out=shift_hh[:], in_=beta_hh.partition_broadcast(P))
+        nc.gpsimd.dma_start(out=gain_c[:], in_=gamma_c.partition_broadcast(P))
+        nc.gpsimd.dma_start(out=shift_c[:], in_=beta_c.partition_broadcast(P))
         nc.gpsimd.tensor_tensor(out=shift[:], in0=shift_ih[:], in1=shift_hh[:], op=ALU.add)
 
         grouped = {}
@@ -140,6 +143,7 @@ def tile_layernormlstmcell_kernel(
         cell = {}
         cell_sum = {}
         cell_neg_mean = {}
+        cell_var_eps = {}
         cell_rstd = {}
         cell_norm = {}
         cell_tanh = {}
@@ -210,20 +214,23 @@ def tile_layernormlstmcell_kernel(
                 accum_out=sq_sums[t][:, o, j : j + 1],
             )
 
-        def inverse_std(total, n, name):
-            var_eps = work4.tile([P, 1], F32, name=name + "_var")
-            nc.gpsimd.tensor_scalar(
-                out=var_eps[:], in0=total[:], scalar1=1.0 / n, scalar2=EPS, op0=ALU.mult, op1=ALU.add
-            )
+        def inverse_root(var_eps, name):
             result = work4.tile([P, 1], F32, name=name)
             nc.gpsimd.tensor_tensor(out=result[:], in0=var_eps[:], in1=neg_half[:], op=ALU.pow)
             return result
 
         def gate_rstd(t, o):
-            total = work4.tile([P, 1], F32, name="sq_total")
+            var_eps = work4.tile([P, 1], F32, name="var_eps")
             scrap = work2.tile([P, PRODUCT_BANKS], F32, name="scrap_total")
-            nc.scalar.activation(out=scrap[:], in_=sq_sums[t][:, o, :], func=ACT.Copy, accum_out=total[:])
-            rstd[t, o] = inverse_std(total, GATES, "rstd")
+            nc.scalar.activation(
+                out=scrap[:],
+                in_=sq_sums[t][:, o, :],
+                func=ACT.Copy,
+                scale=1.0 / GATES,
+                bias=EPS / PRODUCT_BANKS,
+                accum_out=var_eps[:],
+            )
+            rstd[t, o] = inverse_root(var_eps, "rstd")
 
         def centre_and_gain(t, bank):
             o, j = divmod(bank, PRODUCT_BANKS)
@@ -272,18 +279,18 @@ def tile_layernormlstmcell_kernel(
             nc.scalar.activation(out=act_g[t][:], in_=centred[t][1][:, HALF : HALF + HID], func=ACT.Tanh)
 
         def squash_o(t):
-            act_o[t] = work3.tile([P, HID], F32, name="act_o")
+            act_o[t] = work4.tile([P, HID], F32, name="act_o")
             nc.scalar.activation(out=act_o[t][:], in_=centred[t][1][:, HALF + HID : GATES], func=ACT.Sigmoid)
 
         def keep_old(t):
             keep_part[t] = work2.tile([P, HID], F32, name="keep_part")
-            nc.vector.tensor_tensor(
+            nc.gpsimd.tensor_tensor(
                 out=keep_part[t][:], in0=act_if[t][:, HID:HALF], in1=c_sb[:, t, :], op=ALU.mult
             )
 
         def take_new(t):
             new_part[t] = work2.tile([P, HID], F32, name="new_part")
-            nc.vector.tensor_tensor(
+            nc.gpsimd.tensor_tensor(
                 out=new_part[t][:], in0=act_if[t][:, 0:HID], in1=act_g[t][:], op=ALU.mult
             )
 
@@ -314,7 +321,13 @@ def tile_layernormlstmcell_kernel(
                 scale=1.0,
                 accum_out=total[:],
             )
-            cell_rstd[t] = inverse_std(total, HID, "cell_rstd")
+            cell_var_eps[t] = work3.tile([P, 1], F32, name="cell_var_eps")
+            nc.scalar.activation(
+                out=cell_var_eps[t][:], in_=total[:], func=ACT.Copy, scale=1.0 / HID, bias=EPS
+            )
+
+        def cell_power(t):
+            cell_rstd[t] = inverse_root(cell_var_eps[t], "cell_rstd")
 
         def cell_centre_and_gain(t):
             cell_norm[t] = work3.tile([P, HID], F32, name="cell_norm")
@@ -343,15 +356,18 @@ def tile_layernormlstmcell_kernel(
 
         def hidden(t):
             h_new = work3.tile([P, HID], F32, name="h_new")
-            nc.vector.tensor_tensor(out=h_new[:], in0=act_o[t][:], in1=cell_tanh[t][:], op=ALU.mult)
+            nc.gpsimd.tensor_tensor(out=h_new[:], in0=act_o[t][:], in1=cell_tanh[t][:], op=ALU.mult)
             nc.sync.dma_start(out=h_out[:, t, :], in_=h_new[:])
 
         def live(t):
             return 0 <= t < TILES
 
-        for t in range(-4, TILES + 1):
+        for t in range(-4, TILES + 3):
+            if live(t - 2):
+                cell_power(t - 2)
             if live(t - 1):
-                cell_stats(t - 1)
+                keep_old(t - 1)
+                take_new(t - 1)
             for bank in range(BANKS):
                 if live(t):
                     centre_and_gain(t, bank)
@@ -359,8 +375,12 @@ def tile_layernormlstmcell_kernel(
                 if live(later_t):
                     product_pass(later_t, later_bank)
                     square(later_t, later_bank)
-                    if later_bank % PRODUCT_BANKS == PRODUCT_BANKS - 1:
-                        gate_rstd(later_t, later_bank // PRODUCT_BANKS)
+                    if later_bank == BANKS - 1:
+                        gate_rstd(later_t, 1)
+            if live(t - 3):
+                hidden(t - 3)
+            if live(t + 1):
+                gate_rstd(t + 1, 0)
 
             if live(t + 2):
                 mean(t + 2, mean_passes(t + 2))
@@ -368,24 +388,22 @@ def tile_layernormlstmcell_kernel(
                 turn(t + 4)
             if live(t):
                 scale_and_shift(t, 0)
-                scale_and_shift(t, 1)
-            if live(t - 1):
-                cell_centre_and_gain(t - 1)
+            if live(t - 2):
+                cell_centre_and_gain(t - 2)
             if live(t):
                 scale_and_add(t, 0)
                 squash_if(t)
+                scale_and_shift(t, 1)
+            if live(t - 1):
+                new_cell(t - 1)
+                cell_stats(t - 1)
+            if live(t):
                 scale_and_add(t, 1)
                 squash_g(t)
-            if live(t - 1):
-                cell_scale_and_shift(t - 1)
-                squash_cell(t - 1)
+            if live(t - 2):
+                cell_scale_and_shift(t - 2)
+                squash_cell(t - 2)
             if live(t):
                 squash_o(t)
-                keep_old(t)
-                take_new(t)
-            if live(t - 1):
-                hidden(t - 1)
-            if live(t):
-                new_cell(t)
             if live(t + 3):
                 quantise(t + 3)

@@ -22,7 +22,7 @@ BANK = 512
 HALF = 2 * BANK
 PRODUCT_BANKS = GATES // BANK
 BANKS = 2 * PRODUCT_BANKS
-AHEAD = 6
+AHEAD = 7
 TILES = BATCH // P
 EPS = 1e-5
 
@@ -55,8 +55,7 @@ def tile_layernormlstmcell_kernel(
         work3 = ctx.enter_context(tc.tile_pool(name="work3", bufs=3))
         work4 = ctx.enter_context(tc.tile_pool(name="work4", bufs=4))
         ps_prod = ctx.enter_context(tc.psum_pool(name="ps_prod", bufs=AHEAD))
-        ps_sum = ctx.enter_context(tc.psum_pool(name="ps_sum", bufs=1))
-        ps_turn = ctx.enter_context(tc.psum_pool(name="ps_turn", bufs=1))
+        ps_side = ctx.enter_context(tc.psum_pool(name="ps_side", bufs=1))
 
         rows_sb = [
             keep.tile([P, TILES, K], BF16, name="x_sb"),
@@ -83,14 +82,14 @@ def tile_layernormlstmcell_kernel(
         gain_c = keep.tile([P, HID], BF16)
         shift_c = keep.tile([P, HID], BF16)
         ident = keep.tile([P, P], F32)
-        neg_half = keep.tile([P, 1], F32)
+        neg_half = keep.tile([P, 3], F32)
         warm = keep.tile([P, 1], F32)
 
         for plane in w_scales:
             nc.vector.memset(plane[:].bitcast(I32), 0)
         nc.vector.memset(neg_half[:], -0.5)
         masks.make_identity(nc, ident[:])
-        nc.scalar.activation(out=warm[:], in_=neg_half[:], func=ACT.Sigmoid)
+        nc.scalar.activation(out=warm[:], in_=neg_half[:, 0:1], func=ACT.Sigmoid)
 
         rows_dram = [
             x.rearrange("(p t) k -> p t k", t=TILES),
@@ -132,6 +131,7 @@ def tile_layernormlstmcell_kernel(
         grouped = {}
         neg_mean = {}
         sq_sums = {}
+        var_eps = {}
         rstd = {}
         products = {}
         centred = {}
@@ -143,8 +143,6 @@ def tile_layernormlstmcell_kernel(
         cell = {}
         cell_sum = {}
         cell_neg_mean = {}
-        cell_var_eps = {}
-        cell_rstd = {}
         cell_norm = {}
         cell_tanh = {}
 
@@ -160,7 +158,7 @@ def tile_layernormlstmcell_kernel(
             )
 
         def turn(t):
-            turned = ps_turn.tile([P, 4, P], F32)
+            turned = ps_side.tile([P, 4, P], F32, tag="side")
             for o in range(2):
                 words = rows_sb[o][:, t, :].bitcast(F32)
                 for u in range(2):
@@ -178,7 +176,7 @@ def tile_layernormlstmcell_kernel(
 
         def mean_passes(t):
             blocks = GATES // P
-            sums = ps_sum.tile([P, 2, P], F32)
+            sums = ps_side.tile([P, 2, P], F32, tag="side")
             for o in range(2):
                 for c in range(blocks):
                     mx_pass(sums[:, o, :], t, o, c * P, P, c == 0, c == blocks - 1)
@@ -214,13 +212,12 @@ def tile_layernormlstmcell_kernel(
                 accum_out=sq_sums[t][:, o, j : j + 1],
             )
 
-        def inverse_root(var_eps, name):
-            result = work4.tile([P, 1], F32, name=name)
-            nc.gpsimd.tensor_tensor(out=result[:], in0=var_eps[:], in1=neg_half[:], op=ALU.pow)
-            return result
+        def var_eps_column(r, column):
+            if r not in var_eps:
+                var_eps[r] = work3.tile([P, 3], F32, name="var_eps")
+            return var_eps[r][:, column : column + 1]
 
-        def gate_rstd(t, o):
-            var_eps = work4.tile([P, 1], F32, name="var_eps")
+        def gate_var(t, o):
             scrap = work2.tile([P, PRODUCT_BANKS], F32, name="scrap_total")
             nc.scalar.activation(
                 out=scrap[:],
@@ -228,9 +225,19 @@ def tile_layernormlstmcell_kernel(
                 func=ACT.Copy,
                 scale=1.0 / GATES,
                 bias=EPS / PRODUCT_BANKS,
-                accum_out=var_eps[:],
+                accum_out=var_eps_column(t, o),
             )
-            rstd[t, o] = inverse_root(var_eps, "rstd")
+
+        def power(r):
+            first = 0 if live(r) else 2
+            last = 3 if live(r - 2) else 2
+            rstd[r] = work3.tile([P, 3], F32, name="rstd")
+            nc.gpsimd.tensor_tensor(
+                out=rstd[r][:, first:last],
+                in0=var_eps[r][:, first:last],
+                in1=neg_half[:, first:last],
+                op=ALU.pow,
+            )
 
         def centre_and_gain(t, bank):
             o, j = divmod(bank, PRODUCT_BANKS)
@@ -253,7 +260,7 @@ def tile_layernormlstmcell_kernel(
             nc.vector.scalar_tensor_tensor(
                 out=centred[t][0][:, cols],
                 in0=centred[t][0][:, cols],
-                scalar=rstd[t, 0][:],
+                scalar=rstd[t][:, 0:1],
                 in1=shift[:, cols],
                 op0=ALU.mult,
                 op1=ALU.add,
@@ -264,7 +271,7 @@ def tile_layernormlstmcell_kernel(
             nc.vector.scalar_tensor_tensor(
                 out=centred[t][1][:, cols],
                 in0=centred[t][1][:, cols],
-                scalar=rstd[t, 1][:],
+                scalar=rstd[t][:, 1:2],
                 in1=centred[t][0][:, cols],
                 op0=ALU.mult,
                 op1=ALU.add,
@@ -282,15 +289,15 @@ def tile_layernormlstmcell_kernel(
             act_o[t] = work4.tile([P, HID], F32, name="act_o")
             nc.scalar.activation(out=act_o[t][:], in_=centred[t][1][:, HALF + HID : GATES], func=ACT.Sigmoid)
 
-        def keep_old(t):
+        def keep_old(engine, t):
             keep_part[t] = work2.tile([P, HID], F32, name="keep_part")
-            nc.gpsimd.tensor_tensor(
+            engine.tensor_tensor(
                 out=keep_part[t][:], in0=act_if[t][:, HID:HALF], in1=c_sb[:, t, :], op=ALU.mult
             )
 
-        def take_new(t):
+        def take_new(engine, t):
             new_part[t] = work2.tile([P, HID], F32, name="new_part")
-            nc.gpsimd.tensor_tensor(
+            engine.tensor_tensor(
                 out=new_part[t][:], in0=act_if[t][:, 0:HID], in1=act_g[t][:], op=ALU.mult
             )
 
@@ -321,13 +328,9 @@ def tile_layernormlstmcell_kernel(
                 scale=1.0,
                 accum_out=total[:],
             )
-            cell_var_eps[t] = work3.tile([P, 1], F32, name="cell_var_eps")
             nc.scalar.activation(
-                out=cell_var_eps[t][:], in_=total[:], func=ACT.Copy, scale=1.0 / HID, bias=EPS
+                out=var_eps_column(t + 2, 2), in_=total[:], func=ACT.Copy, scale=1.0 / HID, bias=EPS
             )
-
-        def cell_power(t):
-            cell_rstd[t] = inverse_root(cell_var_eps[t], "cell_rstd")
 
         def cell_centre_and_gain(t):
             cell_norm[t] = work3.tile([P, HID], F32, name="cell_norm")
@@ -344,7 +347,7 @@ def tile_layernormlstmcell_kernel(
             nc.vector.scalar_tensor_tensor(
                 out=cell_norm[t][:],
                 in0=cell_norm[t][:],
-                scalar=cell_rstd[t][:],
+                scalar=rstd[t + 2][:, 2:3],
                 in1=shift_c[:],
                 op0=ALU.mult,
                 op1=ALU.add,
@@ -354,20 +357,19 @@ def tile_layernormlstmcell_kernel(
             cell_tanh[t] = work2.tile([P, HID], F32, name="cell_tanh")
             nc.scalar.activation(out=cell_tanh[t][:], in_=cell_norm[t][:], func=ACT.Tanh)
 
-        def hidden(t):
+        def hidden(engine, t):
             h_new = work3.tile([P, HID], F32, name="h_new")
-            nc.gpsimd.tensor_tensor(out=h_new[:], in0=act_o[t][:], in1=cell_tanh[t][:], op=ALU.mult)
+            engine.tensor_tensor(out=h_new[:], in0=act_o[t][:], in1=cell_tanh[t][:], op=ALU.mult)
             nc.sync.dma_start(out=h_out[:, t, :], in_=h_new[:])
 
         def live(t):
             return 0 <= t < TILES
 
         for t in range(-4, TILES + 3):
-            if live(t - 2):
-                cell_power(t - 2)
+            helper = nc.gpsimd if live(t) else nc.vector
             if live(t - 1):
-                keep_old(t - 1)
-                take_new(t - 1)
+                keep_old(helper, t - 1)
+                take_new(helper, t - 1)
             for bank in range(BANKS):
                 if live(t):
                     centre_and_gain(t, bank)
@@ -376,11 +378,13 @@ def tile_layernormlstmcell_kernel(
                     product_pass(later_t, later_bank)
                     square(later_t, later_bank)
                     if later_bank == BANKS - 1:
-                        gate_rstd(later_t, 1)
+                        gate_var(later_t, 1)
+            if live(t) or live(t - 2):
+                power(t)
             if live(t - 3):
-                hidden(t - 3)
+                hidden(helper, t - 3)
             if live(t + 1):
-                gate_rstd(t + 1, 0)
+                gate_var(t + 1, 0)
 
             if live(t + 2):
                 mean(t + 2, mean_passes(t + 2))

@@ -22,7 +22,7 @@ BANK = 512
 HALF = 2 * BANK
 PRODUCT_BANKS = GATES // BANK
 BANKS = 2 * PRODUCT_BANKS
-AHEAD = 7
+AHEAD = 5
 TILES = BATCH // P
 EPS = 1e-5
 
@@ -56,6 +56,7 @@ def tile_layernormlstmcell_kernel(
         work4 = ctx.enter_context(tc.tile_pool(name="work4", bufs=4))
         ps_prod = ctx.enter_context(tc.psum_pool(name="ps_prod", bufs=AHEAD))
         ps_side = ctx.enter_context(tc.psum_pool(name="ps_side", bufs=1))
+        ps_col = ctx.enter_context(tc.psum_pool(name="ps_col", bufs=2))
 
         rows_sb = [
             keep.tile([P, TILES, K], BF16, name="x_sb"),
@@ -128,16 +129,20 @@ def tile_layernormlstmcell_kernel(
         nc.gpsimd.dma_start(out=shift_c[:], in_=beta_c.partition_broadcast(P))
         nc.gpsimd.tensor_tensor(out=shift[:], in0=shift_ih[:], in1=shift_hh[:], op=ALU.add)
 
+        turned = {}
         grouped = {}
+        sums = {}
+        gate_bank = {}
         neg_mean = {}
         sq_sums = {}
         var_eps = {}
         rstd = {}
         products = {}
         centred = {}
-        act_if = {}
+        act_i = {}
         act_g = {}
-        act_o = {}
+        act_fo = {}
+        new_turned = {}
         keep_part = {}
         new_part = {}
         cell = {}
@@ -158,15 +163,17 @@ def tile_layernormlstmcell_kernel(
             )
 
         def turn(t):
-            turned = ps_side.tile([P, 4, P], F32, tag="side")
+            turned[t] = ps_side.tile([P, 4, P], F32, name="turned", tag="side")
             for o in range(2):
                 words = rows_sb[o][:, t, :].bitcast(F32)
                 for u in range(2):
-                    nc.tensor.transpose(turned[:, 2 * o + u, :], words[:, u : K // 2 : 2], ident[:])
+                    nc.tensor.transpose(turned[t][:, 2 * o + u, :], words[:, u : K // 2 : 2], ident[:])
+
+        def regroup(t):
             grouped[t] = work2.tile([P, 2 * P * 4], BF16, name="grouped", align_bytes=64)
             nc.scalar.copy(
                 out=grouped[t][:].bitcast(F32).rearrange("p (o b u) -> p o b u", o=2, u=2),
-                in_=turned[:].rearrange("p (o u) b -> p o b u", u=2),
+                in_=turned[t][:].rearrange("p (o u) b -> p o b u", u=2),
             )
 
         def quantise(t):
@@ -174,26 +181,24 @@ def tile_layernormlstmcell_kernel(
                 out=a_words[:, t, :].bitcast(FP8X4), scales=a_scales[:, t, :], in_=grouped[t][:]
             )
 
-        def mean_passes(t):
+        def mean_passes(t, o):
             blocks = GATES // P
-            sums = ps_side.tile([P, 2, P], F32, tag="side")
-            for o in range(2):
-                for c in range(blocks):
-                    mx_pass(sums[:, o, :], t, o, c * P, P, c == 0, c == blocks - 1)
-            return sums
+            sums[t, o] = ps_side.tile([P, P], F32, name="sums", tag="side")
+            for c in range(blocks):
+                mx_pass(sums[t, o][:], t, o, c * P, P, c == 0, c == blocks - 1)
 
-        def mean(t, sums):
-            neg_mean[t] = work3.tile([P, 2], F32, name="neg_mean")
-            for o in range(2):
-                scrap = work2.tile([P, P], F32, name="scrap_mean")
-                nc.scalar.activation(
-                    out=scrap[:],
-                    in_=sums[:, o, :],
-                    func=ACT.Copy,
-                    scale=-1.0 / GATES,
-                    accum_out=neg_mean[t][:, o : o + 1],
-                )
-            sq_sums[t] = work3.tile([P, 2, PRODUCT_BANKS], F32, name="sq_sums")
+        def mean(t, o):
+            if o == 0:
+                neg_mean[t] = work3.tile([P, 2], F32, name="neg_mean")
+                sq_sums[t] = work3.tile([P, 2, PRODUCT_BANKS], F32, name="sq_sums")
+            scrap = work2.tile([P, P], F32, name="scrap_mean")
+            nc.scalar.activation(
+                out=scrap[:],
+                in_=sums[t, o][:],
+                func=ACT.Copy,
+                scale=-1.0 / GATES,
+                accum_out=neg_mean[t][:, o : o + 1],
+            )
 
         def product_pass(t, bank):
             o, j = divmod(bank, PRODUCT_BANKS)
@@ -255,51 +260,82 @@ def tile_layernormlstmcell_kernel(
                 op1=ALU.mult,
             )
 
-        def scale_and_shift(t, half):
-            cols = slice(half * HALF, (half + 1) * HALF)
-            nc.vector.scalar_tensor_tensor(
-                out=centred[t][0][:, cols],
-                in0=centred[t][0][:, cols],
-                scalar=rstd[t][:, 0:1],
-                in1=shift[:, cols],
+        def pair(ap, first):
+            return ap.rearrange("p (g n) -> p g n", g=4)[:, first::2, :]
+
+        def scale_ig(t, o):
+            nc.vector.tensor_scalar(
+                out=pair(centred[t][o][:], 0),
+                in0=pair(centred[t][o][:], 0),
+                scalar1=rstd[t][:, o : o + 1],
+                scalar2=None,
                 op0=ALU.mult,
-                op1=ALU.add,
             )
 
-        def scale_and_add(t, half):
-            cols = slice(half * HALF, (half + 1) * HALF)
-            nc.vector.scalar_tensor_tensor(
-                out=centred[t][1][:, cols],
-                in0=centred[t][1][:, cols],
-                scalar=rstd[t][:, 1:2],
-                in1=centred[t][0][:, cols],
-                op0=ALU.mult,
-                op1=ALU.add,
-            )
+        def turned_gate(t, gate):
+            bank = ps_col.tile([P, HID // P, P], F32, tag="col")
+            gate_bank[t, gate] = bank
+            for jb in range(HID // P):
+                cols = slice(gate * HID + jb * P, gate * HID + (jb + 1) * P)
+                terms = (shift[:, cols], centred[t][0][:, cols], centred[t][1][:, cols])
+                for n, term in enumerate(terms):
+                    nc.tensor.matmul(
+                        out=bank[:, jb, :],
+                        lhsT=term,
+                        rhs=ident[:],
+                        is_transpose=True,
+                        start=n == 0,
+                        stop=n == len(terms) - 1,
+                    )
 
-        def squash_if(t):
-            act_if[t] = work2.tile([P, HALF], F32, name="act_if")
-            nc.scalar.activation(out=act_if[t][:], in_=centred[t][1][:, 0:HALF], func=ACT.Sigmoid)
+        def squash_i(t):
+            bank = gate_bank[t, 0]
+            act_i[t] = work2.tile([P, HID], F32, name="act_i")
+            nc.scalar.activation(out=act_i[t][:], in_=bank[:].rearrange("p a b -> p (a b)"), func=ACT.Sigmoid)
 
         def squash_g(t):
+            bank = gate_bank[t, 2]
             act_g[t] = work2.tile([P, HID], F32, name="act_g")
-            nc.scalar.activation(out=act_g[t][:], in_=centred[t][1][:, HALF : HALF + HID], func=ACT.Tanh)
+            nc.scalar.activation(out=act_g[t][:], in_=bank[:].rearrange("p a b -> p (a b)"), func=ACT.Tanh)
 
-        def squash_o(t):
-            act_o[t] = work4.tile([P, HID], F32, name="act_o")
-            nc.scalar.activation(out=act_o[t][:], in_=centred[t][1][:, HALF + HID : GATES], func=ACT.Sigmoid)
+        def scale_and_shift(t):
+            nc.vector.scalar_tensor_tensor(
+                out=pair(centred[t][0][:], 1),
+                in0=pair(centred[t][0][:], 1),
+                scalar=rstd[t][:, 0:1],
+                in1=pair(shift[:], 1),
+                op0=ALU.mult,
+                op1=ALU.add,
+            )
+
+        def scale_and_add(t):
+            nc.vector.scalar_tensor_tensor(
+                out=pair(centred[t][1][:], 1),
+                in0=pair(centred[t][1][:], 1),
+                scalar=rstd[t][:, 1:2],
+                in1=pair(centred[t][0][:], 1),
+                op0=ALU.mult,
+                op1=ALU.add,
+            )
+
+        def squash_fo(t):
+            act_fo[t] = work4.tile([P, 2, HID], F32, name="act_fo")
+            nc.scalar.activation(out=act_fo[t][:], in_=pair(centred[t][1][:], 1), func=ACT.Sigmoid)
 
         def keep_old(engine, t):
             keep_part[t] = work2.tile([P, HID], F32, name="keep_part")
             engine.tensor_tensor(
-                out=keep_part[t][:], in0=act_if[t][:, HID:HALF], in1=c_sb[:, t, :], op=ALU.mult
+                out=keep_part[t][:], in0=act_fo[t][:, 0, :], in1=c_sb[:, t, :], op=ALU.mult
             )
 
         def take_new(engine, t):
-            new_part[t] = work2.tile([P, HID], F32, name="new_part")
-            engine.tensor_tensor(
-                out=new_part[t][:], in0=act_if[t][:, 0:HID], in1=act_g[t][:], op=ALU.mult
-            )
+            new_turned[t] = work2.tile([P, HID], F32, name="new_turned")
+            engine.tensor_tensor(out=new_turned[t][:], in0=act_i[t][:], in1=act_g[t][:], op=ALU.mult)
+
+        def turn_back(t):
+            new_part[t] = ps_col.tile([P, HID // P, P], F32, name="new_part", tag="col")
+            for jb in range(HID // P):
+                nc.tensor.transpose(new_part[t][:, jb, :], new_turned[t][:, jb * P : (jb + 1) * P], ident[:])
 
         def new_cell(t):
             cell[t] = work3.tile([P, HID], F32, name="cell")
@@ -308,7 +344,7 @@ def tile_layernormlstmcell_kernel(
                 out=cell[t][:],
                 in0=keep_part[t][:],
                 scalar=1.0,
-                in1=new_part[t][:],
+                in1=new_part[t][:].rearrange("p a b -> p (a b)"),
                 op0=ALU.mult,
                 op1=ALU.add,
                 accum_out=cell_sum[t][:],
@@ -359,7 +395,7 @@ def tile_layernormlstmcell_kernel(
 
         def hidden(engine, t):
             h_new = work3.tile([P, HID], F32, name="h_new")
-            engine.tensor_tensor(out=h_new[:], in0=act_o[t][:], in1=cell_tanh[t][:], op=ALU.mult)
+            engine.tensor_tensor(out=h_new[:], in0=act_fo[t][:, 1, :], in1=cell_tanh[t][:], op=ALU.mult)
             nc.sync.dma_start(out=h_out[:, t, :], in_=h_new[:])
 
         def live(t):
@@ -368,8 +404,10 @@ def tile_layernormlstmcell_kernel(
         for t in range(-4, TILES + 3):
             helper = nc.gpsimd if live(t) else nc.vector
             if live(t - 1):
-                keep_old(helper, t - 1)
                 take_new(helper, t - 1)
+                keep_old(helper, t - 1)
+            if live(t - 3):
+                hidden(helper, t - 3)
             for bank in range(BANKS):
                 if live(t):
                     centre_and_gain(t, bank)
@@ -377,37 +415,45 @@ def tile_layernormlstmcell_kernel(
                 if live(later_t):
                     product_pass(later_t, later_bank)
                     square(later_t, later_bank)
-                    if later_bank == BANKS - 1:
-                        gate_var(later_t, 1)
-            if live(t) or live(t - 2):
-                power(t)
-            if live(t - 3):
-                hidden(helper, t - 3)
-            if live(t + 1):
-                gate_var(t + 1, 0)
+                    if later_bank % PRODUCT_BANKS == PRODUCT_BANKS - 1:
+                        gate_var(later_t, later_bank // PRODUCT_BANKS)
+                if later_bank == BANKS - 1 and (live(t) or live(t - 2)):
+                    power(t)
+                if bank == 3 and live(t - 1):
+                    turn_back(t - 1)
 
             if live(t + 2):
-                mean(t + 2, mean_passes(t + 2))
-            if live(t + 4):
-                turn(t + 4)
+                mean_passes(t + 2, 0)
             if live(t):
-                scale_and_shift(t, 0)
-            if live(t - 2):
-                cell_centre_and_gain(t - 2)
+                scale_ig(t, 0)
+                scale_ig(t, 1)
+            if live(t + 2):
+                mean(t + 2, 0)
             if live(t):
-                scale_and_add(t, 0)
-                squash_if(t)
-                scale_and_shift(t, 1)
+                turned_gate(t, 0)
             if live(t - 1):
                 new_cell(t - 1)
+            if live(t):
+                turned_gate(t, 2)
+            if live(t - 1):
                 cell_stats(t - 1)
             if live(t):
-                scale_and_add(t, 1)
+                squash_i(t)
                 squash_g(t)
+                scale_and_shift(t)
+            if live(t - 2):
+                cell_centre_and_gain(t - 2)
+            if live(t + 4):
+                turn(t + 4)
+                regroup(t + 4)
+            if live(t):
+                scale_and_add(t)
+                squash_fo(t)
             if live(t - 2):
                 cell_scale_and_shift(t - 2)
                 squash_cell(t - 2)
-            if live(t):
-                squash_o(t)
+            if live(t + 2):
+                mean_passes(t + 2, 1)
+                mean(t + 2, 1)
             if live(t + 3):
                 quantise(t + 3)

@@ -110,10 +110,10 @@ def tile_layernormlstmcell_kernel(
         def load_rows(o, first, last):
             nc.sync.dma_start(out=rows_sb[o][:, first:last, :], in_=rows_dram[o][:, first:last, :])
 
-        load_scales(0, W_ih_scales)
         load_rows(0, 0, 2)
-        nc.sync.dma_start(out=w_words[0][:].bitcast(I32), in_=W_ih_words[0].bitcast(I32))
         load_rows(1, 0, 2)
+        nc.sync.dma_start(out=w_words[0][:].bitcast(I32), in_=W_ih_words[0].bitcast(I32))
+        load_scales(0, W_ih_scales)
         nc.sync.dma_start(out=w_words[1][:].bitcast(I32), in_=W_hh_words[0].bitcast(I32))
         load_scales(1, W_hh_scales)
         for first, last in ((2, 4), (4, 8), (8, TILES)):
@@ -401,7 +401,28 @@ def tile_layernormlstmcell_kernel(
         def live(t):
             return 0 <= t < TILES
 
-        for t in range(-4, TILES + 3):
+        turn(0)
+        regroup(0)
+        quantise(0)
+        turn(1)
+        regroup(1)
+        quantise(1)
+        for o in range(2):
+            mean_passes(0, o)
+            mean(0, o)
+            for bank in range(o * PRODUCT_BANKS, min((o + 1) * PRODUCT_BANKS, AHEAD)):
+                product_pass(0, bank)
+                square(0, bank)
+            if (o + 1) * PRODUCT_BANKS <= AHEAD:
+                gate_var(0, o)
+        for o in range(2):
+            mean_passes(1, o)
+            mean(1, o)
+        for t in (2, 3):
+            turn(t)
+            regroup(t)
+
+        for t in range(0, TILES + 3):
             helper = nc.gpsimd if live(t) else nc.vector
             if live(t - 1):
                 take_new(helper, t - 1)
@@ -422,6 +443,8 @@ def tile_layernormlstmcell_kernel(
                 if bank == 3 and live(t - 1):
                     turn_back(t - 1)
 
+            if t == 0:
+                quantise(2)
             if live(t + 2):
                 mean_passes(t + 2, 0)
             if live(t):

@@ -447,6 +447,8 @@ def tile_layernormlstmcell_kernel(
                 quantise(2)
             if live(t + 2):
                 mean_passes(t + 2, 0)
+            if live(t - 1):
+                new_cell(t - 1)
             if live(t):
                 scale_ig(t, 0)
                 scale_ig(t, 1)
@@ -454,9 +456,6 @@ def tile_layernormlstmcell_kernel(
                 mean(t + 2, 0)
             if live(t):
                 turned_gate(t, 0)
-            if live(t - 1):
-                new_cell(t - 1)
-            if live(t):
                 turned_gate(t, 2)
             if live(t - 1):
                 cell_stats(t - 1)

@@ -77,8 +77,8 @@ def tile_layernormlstmcell_kernel(
             keep.tile([P, GATES], BF16, name="gain_ih"),
             keep.tile([P, GATES], BF16, name="gain_hh"),
         ]
-        shift_ih = keep.tile([P, GATES], BF16)
-        shift_hh = keep.tile([P, GATES], BF16)
+        shift_rows = keep.tile([P, GATES], BF16)
+        pick_two = keep.tile([P, P], BF16)
         shift = keep.tile([P, GATES], F32)
         gain_c = keep.tile([P, HID], BF16)
         shift_c = keep.tile([P, HID], BF16)
@@ -89,6 +89,9 @@ def tile_layernormlstmcell_kernel(
         for plane in w_scales:
             nc.vector.memset(plane[:].bitcast(I32), 0)
         nc.vector.memset(neg_half[:], -0.5)
+        nc.vector.memset(shift_rows[:], 0.0)
+        nc.vector.memset(pick_two[:], 0.0)
+        nc.vector.memset(pick_two[0:2, :], 1.0)
         masks.make_identity(nc, ident[:])
         nc.scalar.activation(out=warm[:], in_=neg_half[:, 0:1], func=ACT.Sigmoid)
 
@@ -114,6 +117,8 @@ def tile_layernormlstmcell_kernel(
         load_rows(1, 0, 2)
         nc.sync.dma_start(out=w_words[0][:].bitcast(I32), in_=W_ih_words[0].bitcast(I32))
         load_scales(0, W_ih_scales)
+        nc.sync.dma_start(out=shift_rows[0:1, :], in_=beta_ih.rearrange("(o n) -> o n", o=1))
+        nc.sync.dma_start(out=shift_rows[1:2, :], in_=beta_hh.rearrange("(o n) -> o n", o=1))
         nc.sync.dma_start(out=w_words[1][:].bitcast(I32), in_=W_hh_words[0].bitcast(I32))
         load_scales(1, W_hh_scales)
         for first, last in ((2, 4), (4, 8), (8, TILES)):
@@ -123,11 +128,8 @@ def tile_layernormlstmcell_kernel(
         nc.sync.dma_start(out=c_sb[:, TILES - 2 : TILES, :], in_=c_dram[:, TILES - 2 : TILES, :])
         nc.gpsimd.dma_start(out=gain[0][:], in_=gamma_ih.partition_broadcast(P))
         nc.gpsimd.dma_start(out=gain[1][:], in_=gamma_hh.partition_broadcast(P))
-        nc.gpsimd.dma_start(out=shift_ih[:], in_=beta_ih.partition_broadcast(P))
-        nc.gpsimd.dma_start(out=shift_hh[:], in_=beta_hh.partition_broadcast(P))
         nc.gpsimd.dma_start(out=gain_c[:], in_=gamma_c.partition_broadcast(P))
         nc.gpsimd.dma_start(out=shift_c[:], in_=beta_c.partition_broadcast(P))
-        nc.gpsimd.tensor_tensor(out=shift[:], in0=shift_ih[:], in1=shift_hh[:], op=ALU.add)
 
         turned = {}
         grouped = {}
@@ -272,6 +274,18 @@ def tile_layernormlstmcell_kernel(
                 op0=ALU.mult,
             )
 
+        def spread_shift():
+            for j in range(PRODUCT_BANKS):
+                spread = ps_col.tile([P, BANK], F32, tag="col")
+                nc.tensor.matmul(
+                    out=spread[:],
+                    lhsT=pick_two[:],
+                    rhs=shift_rows[:, j * BANK : (j + 1) * BANK],
+                    start=True,
+                    stop=True,
+                )
+                nc.vector.tensor_copy(out=shift[:, j * BANK : (j + 1) * BANK], in_=spread[:])
+
         def turned_gate(t, gate):
             bank = ps_col.tile([P, HID // P, P], F32, tag="col")
             gate_bank[t, gate] = bank
@@ -407,6 +421,7 @@ def tile_layernormlstmcell_kernel(
         turn(1)
         regroup(1)
         quantise(1)
+        spread_shift()
         for o in range(2):
             mean_passes(0, o)
             mean(0, o)

@@ -22,7 +22,7 @@ BANK = 512
 HALF = 2 * BANK
 PRODUCT_BANKS = GATES // BANK
 BANKS = 2 * PRODUCT_BANKS
-AHEAD = 5
+AHEAD = 4
 TILES = BATCH // P
 EPS = 1e-5
 
@@ -55,7 +55,7 @@ def tile_layernormlstmcell_kernel(
         work3 = ctx.enter_context(tc.tile_pool(name="work3", bufs=3))
         work4 = ctx.enter_context(tc.tile_pool(name="work4", bufs=4))
         ps_prod = ctx.enter_context(tc.psum_pool(name="ps_prod", bufs=AHEAD))
-        ps_side = ctx.enter_context(tc.psum_pool(name="ps_side", bufs=1))
+        ps_side = ctx.enter_context(tc.psum_pool(name="ps_side", bufs=2))
         ps_col = ctx.enter_context(tc.psum_pool(name="ps_col", bufs=2))
 
         rows_sb = [

@@ -86,10 +86,12 @@ def tile_layernormlstmcell_kernel(
         neg_half = keep.tile([P, 3], F32)
         warm = keep.tile([P, 1], F32)
 
+        nc.vector.memset(shift_rows[:].bitcast(I32), 0)
+        nc.scalar.dma_start(out=shift_rows[0:1, :], in_=beta_ih.rearrange("(o n) -> o n", o=1))
+        nc.scalar.dma_start(out=shift_rows[1:2, :], in_=beta_hh.rearrange("(o n) -> o n", o=1))
         for plane in w_scales:
             nc.vector.memset(plane[:].bitcast(I32), 0)
         nc.vector.memset(neg_half[:], -0.5)
-        nc.vector.memset(shift_rows[:], 0.0)
         nc.vector.memset(pick_two[:], 0.0)
         nc.vector.memset(pick_two[0:2, :], 1.0)
         masks.make_identity(nc, ident[:])
@@ -117,8 +119,6 @@ def tile_layernormlstmcell_kernel(
         load_rows(1, 0, 2)
         nc.sync.dma_start(out=w_words[0][:].bitcast(I32), in_=W_ih_words[0].bitcast(I32))
         load_scales(0, W_ih_scales)
-        nc.sync.dma_start(out=shift_rows[0:1, :], in_=beta_ih.rearrange("(o n) -> o n", o=1))
-        nc.sync.dma_start(out=shift_rows[1:2, :], in_=beta_hh.rearrange("(o n) -> o n", o=1))
         nc.sync.dma_start(out=w_words[1][:].bitcast(I32), in_=W_hh_words[0].bitcast(I32))
         load_scales(1, W_hh_scales)
         for first, last in ((2, 4), (4, 8), (8, TILES)):
@@ -276,7 +276,7 @@ def tile_layernormlstmcell_kernel(
 
         def spread_shift():
             for j in range(PRODUCT_BANKS):
-                spread = ps_col.tile([P, BANK], F32, tag="col")
+                spread = ps_prod.tile([P, BANK], F32, name="product")
                 nc.tensor.matmul(
                     out=spread[:],
                     lhsT=pick_two[:],
@@ -284,7 +284,8 @@ def tile_layernormlstmcell_kernel(
                     start=True,
                     stop=True,
                 )
-                nc.vector.tensor_copy(out=shift[:, j * BANK : (j + 1) * BANK], in_=spread[:])
+                copy = nc.vector.tensor_copy if j % 2 == 0 else nc.scalar.copy
+                copy(out=shift[:, j * BANK : (j + 1) * BANK], in_=spread[:])
 
         def turned_gate(t, gate):
             bank = ps_col.tile([P, HID // P, P], F32, tag="col")
@@ -430,12 +431,6 @@ def tile_layernormlstmcell_kernel(
                 square(0, bank)
             if (o + 1) * PRODUCT_BANKS <= AHEAD:
                 gate_var(0, o)
-        for o in range(2):
-            mean_passes(1, o)
-            mean(1, o)
-        for t in (2, 3):
-            turn(t)
-            regroup(t)
 
         for t in range(0, TILES + 3):
             helper = nc.gpsimd if live(t) else nc.vector
@@ -457,6 +452,12 @@ def tile_layernormlstmcell_kernel(
                     power(t)
                 if bank == 3 and live(t - 1):
                     turn_back(t - 1)
+                if t == 0 and bank in (0, 4):
+                    mean_passes(1, bank // PRODUCT_BANKS)
+                    mean(1, bank // PRODUCT_BANKS)
+                if t == 0 and bank in (5, 6):
+                    turn(bank - 3)
+                    regroup(bank - 3)
 
             if t == 0:
                 quantise(2)

@@ -333,9 +333,12 @@ def tile_layernormlstmcell_kernel(
                 op1=ALU.add,
             )
 
-        def squash_fo(t):
+        def squash_f(t):
             act_fo[t] = work4.tile([P, 2, HID], F32, name="act_fo")
-            nc.scalar.activation(out=act_fo[t][:], in_=pair(centred[t][1][:], 1), func=ACT.Sigmoid)
+            nc.scalar.activation(out=act_fo[t][:, 0, :], in_=centred[t][1][:, HID : 2 * HID], func=ACT.Sigmoid)
+
+        def squash_o(t):
+            nc.scalar.activation(out=act_fo[t][:, 1, :], in_=centred[t][1][:, 3 * HID : 4 * HID], func=ACT.Sigmoid)
 
         def keep_old(engine, t):
             keep_part[t] = work2.tile([P, HID], F32, name="keep_part")
@@ -437,7 +440,7 @@ def tile_layernormlstmcell_kernel(
             if live(t - 1):
                 take_new(helper, t - 1)
                 keep_old(helper, t - 1)
-            if live(t - 3):
+            if live(t - 3) and live(t):
                 hidden(helper, t - 3)
             for bank in range(BANKS):
                 if live(t):
@@ -475,6 +478,7 @@ def tile_layernormlstmcell_kernel(
                 turned_gate(t, 2)
             if live(t - 1):
                 cell_stats(t - 1)
+                squash_o(t - 1)
             if live(t):
                 squash_i(t)
                 squash_g(t)
@@ -486,7 +490,7 @@ def tile_layernormlstmcell_kernel(
                 regroup(t + 4)
             if live(t):
                 scale_and_add(t)
-                squash_fo(t)
+                squash_f(t)
             if live(t - 2):
                 cell_scale_and_shift(t - 2)
                 squash_cell(t - 2)
@@ -495,3 +499,5 @@ def tile_layernormlstmcell_kernel(
                 mean(t + 2, 1)
             if live(t + 3):
                 quantise(t + 3)
+            if live(t - 3) and not live(t):
+                hidden(helper, t - 3)

@@ -25,6 +25,7 @@ BANKS = 2 * PRODUCT_BANKS
 AHEAD = 4
 TILES = BATCH // P
 EPS = 1e-5
+PLACE = (0, 2, 1, 3)
 
 FLOPS = 2 * 2 * BATCH * K * GATES
 
@@ -254,7 +255,7 @@ def tile_layernormlstmcell_kernel(
                     work2.tile([P, GATES], F32, name="centred_hh"),
                 ]
             nc.vector.scalar_tensor_tensor(
-                out=centred[t][o][:, j * BANK : (j + 1) * BANK],
+                out=centred[t][o][:, PLACE[j] * BANK : (PLACE[j] + 1) * BANK],
                 in0=products[t, bank][:],
                 scalar=neg_mean[t][:, o : o + 1],
                 in1=gain[o][:, j * BANK : (j + 1) * BANK],
@@ -263,7 +264,7 @@ def tile_layernormlstmcell_kernel(
             )
 
         def pair(ap, first):
-            return ap.rearrange("p (g n) -> p g n", g=4)[:, first::2, :]
+            return ap[:, first * HALF : (first + 1) * HALF]
 
         def scale_ig(t, o):
             nc.vector.tensor_scalar(
@@ -285,13 +286,13 @@ def tile_layernormlstmcell_kernel(
                     stop=True,
                 )
                 copy = nc.vector.tensor_copy if j % 2 == 0 else nc.scalar.copy
-                copy(out=shift[:, j * BANK : (j + 1) * BANK], in_=spread[:])
+                copy(out=shift[:, PLACE[j] * BANK : (PLACE[j] + 1) * BANK], in_=spread[:])
 
         def turned_gate(t, gate):
             bank = ps_col.tile([P, HID // P, P], F32, tag="col")
             gate_bank[t, gate] = bank
             for jb in range(HID // P):
-                cols = slice(gate * HID + jb * P, gate * HID + (jb + 1) * P)
+                cols = slice(PLACE[gate] * HID + jb * P, PLACE[gate] * HID + (jb + 1) * P)
                 terms = (shift[:, cols], centred[t][0][:, cols], centred[t][1][:, cols])
                 for n, term in enumerate(terms):
                     nc.tensor.matmul(
@@ -335,10 +336,10 @@ def tile_layernormlstmcell_kernel(
 
         def squash_f(t):
             act_fo[t] = work4.tile([P, 2, HID], F32, name="act_fo")
-            nc.scalar.activation(out=act_fo[t][:, 0, :], in_=centred[t][1][:, HID : 2 * HID], func=ACT.Sigmoid)
+            nc.scalar.activation(out=act_fo[t][:, 0, :], in_=centred[t][1][:, PLACE[1] * HID : (PLACE[1] + 1) * HID], func=ACT.Sigmoid)
 
         def squash_o(t):
-            nc.scalar.activation(out=act_fo[t][:, 1, :], in_=centred[t][1][:, 3 * HID : 4 * HID], func=ACT.Sigmoid)
+            nc.scalar.activation(out=act_fo[t][:, 1, :], in_=centred[t][1][:, PLACE[3] * HID : (PLACE[3] + 1) * HID], func=ACT.Sigmoid)
 
         def keep_old(engine, t):
             keep_part[t] = work2.tile([P, HID], F32, name="keep_part")

@@ -56,8 +56,7 @@ def tile_layernormlstmcell_kernel(
         work3 = ctx.enter_context(tc.tile_pool(name="work3", bufs=3))
         work4 = ctx.enter_context(tc.tile_pool(name="work4", bufs=4))
         ps_prod = ctx.enter_context(tc.psum_pool(name="ps_prod", bufs=AHEAD))
-        ps_side = ctx.enter_context(tc.psum_pool(name="ps_side", bufs=2))
-        ps_col = ctx.enter_context(tc.psum_pool(name="ps_col", bufs=2))
+        ps_rest = ctx.enter_context(tc.psum_pool(name="ps_rest", bufs=8 - AHEAD))
 
         rows_sb = [
             keep.tile([P, TILES, K], BF16, name="x_sb"),
@@ -166,7 +165,7 @@ def tile_layernormlstmcell_kernel(
             )
 
         def turn(t):
-            turned[t] = ps_side.tile([P, 4, P], F32, name="turned", tag="side")
+            turned[t] = ps_rest.tile([P, 4, P], F32, name="turned", tag="rest")
             for o in range(2):
                 words = rows_sb[o][:, t, :].bitcast(F32)
                 for u in range(2):
@@ -186,7 +185,7 @@ def tile_layernormlstmcell_kernel(
 
         def mean_passes(t, o):
             blocks = GATES // P
-            sums[t, o] = ps_side.tile([P, P], F32, name="sums", tag="side")
+            sums[t, o] = ps_rest.tile([P, P], F32, name="sums", tag="rest")
             for c in range(blocks):
                 mx_pass(sums[t, o][:], t, o, c * P, P, c == 0, c == blocks - 1)
 
@@ -289,7 +288,7 @@ def tile_layernormlstmcell_kernel(
                 copy(out=shift[:, PLACE[j] * BANK : (PLACE[j] + 1) * BANK], in_=spread[:])
 
         def turned_gate(t, gate):
-            bank = ps_col.tile([P, HID // P, P], F32, tag="col")
+            bank = ps_rest.tile([P, HID // P, P], F32, tag="rest")
             gate_bank[t, gate] = bank
             for jb in range(HID // P):
                 cols = slice(PLACE[gate] * HID + jb * P, PLACE[gate] * HID + (jb + 1) * P)
@@ -352,7 +351,7 @@ def tile_layernormlstmcell_kernel(
             engine.tensor_tensor(out=new_turned[t][:], in0=act_i[t][:], in1=act_g[t][:], op=ALU.mult)
 
         def turn_back(t):
-            new_part[t] = ps_col.tile([P, HID // P, P], F32, name="new_part", tag="col")
+            new_part[t] = ps_rest.tile([P, HID // P, P], F32, name="new_part", tag="rest")
             for jb in range(HID // P):
                 nc.tensor.transpose(new_part[t][:, jb, :], new_turned[t][:, jb * P : (jb + 1) * P], ident[:])
 

@@ -468,6 +468,8 @@ def tile_layernormlstmcell_kernel(
                 mean_passes(t + 2, 0)
             if live(t - 1):
                 new_cell(t - 1)
+            if live(t + 3):
+                quantise(t + 3)
             if live(t):
                 scale_ig(t, 0)
                 scale_ig(t, 1)
@@ -497,7 +499,5 @@ def tile_layernormlstmcell_kernel(
             if live(t + 2):
                 mean_passes(t + 2, 1)
                 mean(t + 2, 1)
-            if live(t + 3):
-                quantise(t + 3)
             if live(t - 3) and not live(t):
                 hidden(helper, t - 3)

from contextlib import ExitStack

import concourse.masks as masks
import concourse.mybir as mybir

F32 = mybir.dt.float32
BF16 = mybir.dt.bfloat16
I32 = mybir.dt.int32
U32 = mybir.dt.uint32
U8 = mybir.dt.uint8
FP8X4 = mybir.dt.float8_e4m3fn_x4
FP4X4 = mybir.dt.float4_e2m1fn_x4
ALU = mybir.AluOpType
ACT = mybir.ActivationFunctionType

P = 128
BATCH = 2048
K = 512
GATES = 2048
HID = 512
BANK = 512
HALF = 2 * BANK
PRODUCT_BANKS = GATES // BANK
BANKS = 2 * PRODUCT_BANKS
AHEAD = 4
TILES = BATCH // P
EPS = 1e-5
PLACE = (0, 2, 1, 3)

FLOPS = 2 * 2 * BATCH * K * GATES


def tile_layernormlstmcell_kernel(
    tc,
    x,
    h_prev,
    c_prev,
    W_ih_words,
    W_ih_scales,
    W_hh_words,
    W_hh_scales,
    gamma_ih,
    beta_ih,
    gamma_hh,
    beta_hh,
    gamma_c,
    beta_c,
    out_0,
    out_1,
):
    nc = tc.nc
    with ExitStack() as ctx:
        ctx.enter_context(tc.manual_schedule())
        keep = ctx.enter_context(tc.tile_pool(name="keep", bufs=1))
        work2 = ctx.enter_context(tc.tile_pool(name="work2", bufs=2))
        work3 = ctx.enter_context(tc.tile_pool(name="work3", bufs=3))
        work4 = ctx.enter_context(tc.tile_pool(name="work4", bufs=4))
        ps_prod = ctx.enter_context(tc.psum_pool(name="ps_prod", bufs=AHEAD))
        ps_rest = ctx.enter_context(tc.psum_pool(name="ps_rest", bufs=8 - AHEAD))

        rows_sb = [
            keep.tile([P, TILES, K], BF16, name="x_sb"),
            keep.tile([P, TILES, K], BF16, name="h_sb"),
        ]
        c_sb = keep.tile([P, TILES, HID], BF16)
        w_words = [
            keep.tile([P, 2 * GATES], U8, name="w_ih_words", align_bytes=64),
            keep.tile([P, 2 * GATES], U8, name="w_hh_words", align_bytes=64),
        ]
        w_scales = [
            keep.tile([P, GATES], U8, name="w_ih_plane", align_bytes=64),
            keep.tile([P, GATES], U8, name="w_hh_plane", align_bytes=64),
        ]
        a_words = keep.tile([P, TILES, 2 * P], U32, align_bytes=64)
        a_scales = keep.tile([P, TILES, 2 * P], U8, align_bytes=64)
        gain = [
            keep.tile([P, GATES], BF16, name="gain_ih"),
            keep.tile([P, GATES], BF16, name="gain_hh"),
        ]
        shift_rows = keep.tile([P, GATES], BF16)
        pick_two = keep.tile([P, P], BF16)
        shift = keep.tile([P, GATES], F32)
        gain_c = keep.tile([P, HID], BF16)
        shift_c = keep.tile([P, HID], BF16)
        ident = keep.tile([P, P], F32)
        neg_half = keep.tile([P, 3], F32)
        warm = keep.tile([P, 1], F32)

        nc.vector.memset(shift_rows[:].bitcast(I32), 0)
        nc.scalar.dma_start(out=shift_rows[0:1, :], in_=beta_ih.rearrange("(o n) -> o n", o=1))
        nc.scalar.dma_start(out=shift_rows[1:2, :], in_=beta_hh.rearrange("(o n) -> o n", o=1))
        for plane in w_scales:
            nc.vector.memset(plane[:].bitcast(I32), 0)
        nc.vector.memset(neg_half[:], -0.5)
        nc.vector.memset(pick_two[:], 0.0)
        nc.vector.memset(pick_two[0:2, :], 1.0)
        masks.make_identity(nc, ident[:])
        nc.scalar.activation(out=warm[:], in_=neg_half[:, 0:1], func=ACT.Sigmoid)

        rows_dram = [
            x.rearrange("(p t) k -> p t k", t=TILES),
            h_prev.rearrange("(p t) k -> p t k", t=TILES),
        ]
        c_dram = c_prev.rearrange("(p t) n -> p t n", t=TILES)
        h_out = out_0.rearrange("(p t) n -> p t n", t=TILES)
        c_out = out_1.rearrange("(p t) n -> p t n", t=TILES)

        def load_scales(o, scales):
            for quad in range(4):
                nc.sync.dma_start(
                    out=w_scales[o][32 * quad : 32 * quad + 4, :].bitcast(I32),
                    in_=scales[0, 4 * quad : 4 * quad + 4, :].bitcast(I32),
                )

        def load_rows(o, first, last):
            nc.sync.dma_start(out=rows_sb[o][:, first:last, :], in_=rows_dram[o][:, first:last, :])

        load_rows(0, 0, 2)
        load_rows(1, 0, 2)
        nc.sync.dma_start(out=w_words[0][:].bitcast(I32), in_=W_ih_words[0].bitcast(I32))
        load_scales(0, W_ih_scales)
        nc.sync.dma_start(out=w_words[1][:].bitcast(I32), in_=W_hh_words[0].bitcast(I32))
        load_scales(1, W_hh_scales)
        for first, last in ((2, 4), (4, 8), (8, TILES)):
            load_rows(0, first, last)
            load_rows(1, first, last)
            nc.sync.dma_start(out=c_sb[:, first - 2 : last - 2, :], in_=c_dram[:, first - 2 : last - 2, :])
        nc.sync.dma_start(out=c_sb[:, TILES - 2 : TILES, :], in_=c_dram[:, TILES - 2 : TILES, :])
        nc.gpsimd.dma_start(out=gain[0][:], in_=gamma_ih.partition_broadcast(P))
        nc.gpsimd.dma_start(out=gain[1][:], in_=gamma_hh.partition_broadcast(P))
        nc.gpsimd.dma_start(out=gain_c[:], in_=gamma_c.partition_broadcast(P))
        nc.gpsimd.dma_start(out=shift_c[:], in_=beta_c.partition_broadcast(P))

        turned = {}
        grouped = {}
        sums = {}
        gate_bank = {}
        neg_mean = {}
        sq_sums = {}
        var_eps = {}
        rstd = {}
        products = {}
        centred = {}
        act_i = {}
        act_g = {}
        act_fo = {}
        new_turned = {}
        keep_part = {}
        new_part = {}
        cell = {}
        cell_sum = {}
        cell_neg_mean = {}
        cell_norm = {}
        cell_tanh = {}

        def mx_pass(out, t, o, first_col, n_cols, start, stop):
            nc.tensor.matmul_mx(
                out=out,
                lhsT=a_words[:, t, o * P : (o + 1) * P].bitcast(FP8X4),
                lhsT_scale=a_scales[:, t, o * P : (o + 1) * P],
                rhs=w_words[o][:, 2 * first_col : 2 * (first_col + n_cols)].bitcast(FP4X4),
                rhs_scale=w_scales[o][:, first_col : first_col + n_cols],
                start=start,
                stop=stop,
            )

        def turn(t):
            turned[t] = ps_rest.tile([P, 4, P], F32, name="turned", tag="rest")
            for o in range(2):
                words = rows_sb[o][:, t, :].bitcast(F32)
                for u in range(2):
                    nc.tensor.transpose(turned[t][:, 2 * o + u, :], words[:, u : K // 2 : 2], ident[:])

        def regroup(t):
            grouped[t] = work2.tile([P, 2 * P * 4], BF16, name="grouped", align_bytes=64)
            nc.scalar.copy(
                out=grouped[t][:].bitcast(F32).rearrange("p (o b u) -> p o b u", o=2, u=2),
                in_=turned[t][:].rearrange("p (o u) b -> p o b u", u=2),
            )

        def quantise(t):
            nc.vector.quantize_mx(
                out=a_words[:, t, :].bitcast(FP8X4), scales=a_scales[:, t, :], in_=grouped[t][:]
            )

        def mean_passes(t, o):
            blocks = GATES // P
            sums[t, o] = ps_rest.tile([P, P], F32, name="sums", tag="rest")
            for c in range(blocks):
                mx_pass(sums[t, o][:], t, o, c * P, P, c == 0, c == blocks - 1)

        def mean(t, o):
            if o == 0:
                neg_mean[t] = work3.tile([P, 2], F32, name="neg_mean")
                sq_sums[t] = work3.tile([P, 2, PRODUCT_BANKS], F32, name="sq_sums")
            scrap = work2.tile([P, P], F32, name="scrap_mean")
            nc.scalar.activation(
                out=scrap[:],
                in_=sums[t, o][:],
                func=ACT.Copy,
                scale=-1.0 / GATES,
                accum_out=neg_mean[t][:, o : o + 1],
            )

        def product_pass(t, bank):
            o, j = divmod(bank, PRODUCT_BANKS)
            products[t, bank] = ps_prod.tile([P, BANK], F32, name="product")
            mx_pass(products[t, bank][:], t, o, j * BANK, BANK, True, True)

        def square(t, bank):
            o, j = divmod(bank, PRODUCT_BANKS)
            scrap = work2.tile([P, BANK], F32, name="scrap_square")
            nc.scalar.activation(
                out=scrap[:],
                in_=products[t, bank][:],
                func=ACT.Square,
                bias=neg_mean[t][:, o : o + 1],
                scale=1.0,
                accum_out=sq_sums[t][:, o, j : j + 1],
            )

        def var_eps_column(r, column):
            if r not in var_eps:
                var_eps[r] = work3.tile([P, 3], F32, name="var_eps")
            return var_eps[r][:, column : column + 1]

        def gate_var(t, o):
            scrap = work2.tile([P, PRODUCT_BANKS], F32, name="scrap_total")
            nc.scalar.activation(
                out=scrap[:],
                in_=sq_sums[t][:, o, :],
                func=ACT.Copy,
                scale=1.0 / GATES,
                bias=EPS / PRODUCT_BANKS,
                accum_out=var_eps_column(t, o),
            )

        def power(r):
            first = 0 if live(r) else 2
            last = 3 if live(r - 2) else 2
            rstd[r] = work3.tile([P, 3], F32, name="rstd")
            nc.gpsimd.tensor_tensor(
                out=rstd[r][:, first:last],
                in0=var_eps[r][:, first:last],
                in1=neg_half[:, first:last],
                op=ALU.pow,
            )

        def centre_and_gain(t, bank):
            o, j = divmod(bank, PRODUCT_BANKS)
            if bank == 0:
                centred[t] = [
                    work2.tile([P, GATES], F32, name="centred_ih"),
                    work2.tile([P, GATES], F32, name="centred_hh"),
                ]
            nc.vector.scalar_tensor_tensor(
                out=centred[t][o][:, PLACE[j] * BANK : (PLACE[j] + 1) * BANK],
                in0=products[t, bank][:],
                scalar=neg_mean[t][:, o : o + 1],
                in1=gain[o][:, j * BANK : (j + 1) * BANK],
                op0=ALU.add,
                op1=ALU.mult,
            )

        def pair(ap, first):
            return ap[:, first * HALF : (first + 1) * HALF]

        def scale_ig(t, o):
            nc.vector.tensor_scalar(
                out=pair(centred[t][o][:], 0),
                in0=pair(centred[t][o][:], 0),
                scalar1=rstd[t][:, o : o + 1],
                scalar2=None,
                op0=ALU.mult,
            )

        def spread_shift():
            for j in range(PRODUCT_BANKS):
                spread = ps_prod.tile([P, BANK], F32, name="product")
                nc.tensor.matmul(
                    out=spread[:],
                    lhsT=pick_two[:],
                    rhs=shift_rows[:, j * BANK : (j + 1) * BANK],
                    start=True,
                    stop=True,
                )
                copy = nc.vector.tensor_copy if j % 2 == 0 else nc.scalar.copy
                copy(out=shift[:, PLACE[j] * BANK : (PLACE[j] + 1) * BANK], in_=spread[:])

        def turned_gate(t, gate):
            bank = ps_rest.tile([P, HID // P, P], F32, tag="rest")
            gate_bank[t, gate] = bank
            for jb in range(HID // P):
                cols = slice(PLACE[gate] * HID + jb * P, PLACE[gate] * HID + (jb + 1) * P)
                terms = (shift[:, cols], centred[t][0][:, cols], centred[t][1][:, cols])
                for n, term in enumerate(terms):
                    nc.tensor.matmul(
                        out=bank[:, jb, :],
                        lhsT=term,
                        rhs=ident[:],
                        is_transpose=True,
                        start=n == 0,
                        stop=n == len(terms) - 1,
                    )

        def squash_i(t):
            bank = gate_bank[t, 0]
            act_i[t] = work2.tile([P, HID], F32, name="act_i")
            nc.scalar.activation(out=act_i[t][:], in_=bank[:].rearrange("p a b -> p (a b)"), func=ACT.Sigmoid)

        def squash_g(t):
            bank = gate_bank[t, 2]
            act_g[t] = work2.tile([P, HID], F32, name="act_g")
            nc.scalar.activation(out=act_g[t][:], in_=bank[:].rearrange("p a b -> p (a b)"), func=ACT.Tanh)

        def scale_and_shift(t):
            nc.vector.scalar_tensor_tensor(
                out=pair(centred[t][0][:], 1),
                in0=pair(centred[t][0][:], 1),
                scalar=rstd[t][:, 0:1],
                in1=pair(shift[:], 1),
                op0=ALU.mult,
                op1=ALU.add,
            )

        def scale_and_add(t):
            nc.vector.scalar_tensor_tensor(
                out=pair(centred[t][1][:], 1),
                in0=pair(centred[t][1][:], 1),
                scalar=rstd[t][:, 1:2],
                in1=pair(centred[t][0][:], 1),
                op0=ALU.mult,
                op1=ALU.add,
            )

        def squash_f(t):
            act_fo[t] = work4.tile([P, 2, HID], F32, name="act_fo")
            nc.scalar.activation(out=act_fo[t][:, 0, :], in_=centred[t][1][:, PLACE[1] * HID : (PLACE[1] + 1) * HID], func=ACT.Sigmoid)

        def squash_o(t):
            nc.scalar.activation(out=act_fo[t][:, 1, :], in_=centred[t][1][:, PLACE[3] * HID : (PLACE[3] + 1) * HID], func=ACT.Sigmoid)

        def keep_old(engine, t):
            keep_part[t] = work2.tile([P, HID], F32, name="keep_part")
            engine.tensor_tensor(
                out=keep_part[t][:], in0=act_fo[t][:, 0, :], in1=c_sb[:, t, :], op=ALU.mult
            )

        def take_new(engine, t):
            new_turned[t] = work2.tile([P, HID], F32, name="new_turned")
            engine.tensor_tensor(out=new_turned[t][:], in0=act_i[t][:], in1=act_g[t][:], op=ALU.mult)

        def turn_back(t):
            new_part[t] = ps_rest.tile([P, HID // P, P], F32, name="new_part", tag="rest")
            for jb in range(HID // P):
                nc.tensor.transpose(new_part[t][:, jb, :], new_turned[t][:, jb * P : (jb + 1) * P], ident[:])

        def new_cell(t):
            cell[t] = work3.tile([P, HID], F32, name="cell")
            cell_sum[t] = work3.tile([P, 1], F32, name="cell_sum")
            nc.vector.scalar_tensor_tensor(
                out=cell[t][:],
                in0=keep_part[t][:],
                scalar=1.0,
                in1=new_part[t][:].rearrange("p a b -> p (a b)"),
                op0=ALU.mult,
                op1=ALU.add,
                accum_out=cell_sum[t][:],
            )
            nc.sync.dma_start(out=c_out[:, t, :], in_=cell[t][:])

        def cell_stats(t):
            cell_neg_mean[t] = work3.tile([P, 1], F32, name="cell_neg_mean")
            nc.scalar.mul(out=cell_neg_mean[t][:], in_=cell_sum[t][:], mul=-1.0 / HID)
            scrap = work2.tile([P, BANK], F32, name="scrap_square")
            total = work3.tile([P, 1], F32, name="cell_sq_total")
            nc.scalar.activation(
                out=scrap[:],
                in_=cell[t][:],
                func=ACT.Square,
                bias=cell_neg_mean[t][:],
                scale=1.0,
                accum_out=total[:],
            )
            nc.scalar.activation(
                out=var_eps_column(t + 2, 2), in_=total[:], func=ACT.Copy, scale=1.0 / HID, bias=EPS
            )

        def cell_centre_and_gain(t):
            cell_norm[t] = work3.tile([P, HID], F32, name="cell_norm")
            nc.vector.scalar_tensor_tensor(
                out=cell_norm[t][:],
                in0=cell[t][:],
                scalar=cell_neg_mean[t][:],
                in1=gain_c[:],
                op0=ALU.add,
                op1=ALU.mult,
            )

        def cell_scale_and_shift(t):
            nc.vector.scalar_tensor_tensor(
                out=cell_norm[t][:],
                in0=cell_norm[t][:],
                scalar=rstd[t + 2][:, 2:3],
                in1=shift_c[:],
                op0=ALU.mult,
                op1=ALU.add,
            )

        def squash_cell(t):
            cell_tanh[t] = work2.tile([P, HID], F32, name="cell_tanh")
            nc.scalar.activation(out=cell_tanh[t][:], in_=cell_norm[t][:], func=ACT.Tanh)

        def hidden(engine, t):
            h_new = work3.tile([P, HID], F32, name="h_new")
            engine.tensor_tensor(out=h_new[:], in0=act_fo[t][:, 1, :], in1=cell_tanh[t][:], op=ALU.mult)
            nc.sync.dma_start(out=h_out[:, t, :], in_=h_new[:])

        def live(t):
            return 0 <= t < TILES

        turn(0)
        regroup(0)
        quantise(0)
        turn(1)
        regroup(1)
        quantise(1)
        spread_shift()
        for o in range(2):
            mean_passes(0, o)
            mean(0, o)
            for bank in range(o * PRODUCT_BANKS, min((o + 1) * PRODUCT_BANKS, AHEAD)):
                product_pass(0, bank)
                square(0, bank)
            if (o + 1) * PRODUCT_BANKS <= AHEAD:
                gate_var(0, o)

        for t in range(0, TILES + 3):
            helper = nc.gpsimd if live(t) else nc.vector
            if live(t - 1):
                take_new(helper, t - 1)
                keep_old(helper, t - 1)
            if live(t - 3) and live(t):
                hidden(helper, t - 3)
            for bank in range(BANKS):
                if live(t):
                    centre_and_gain(t, bank)
                later_t, later_bank = t + (bank + AHEAD) // BANKS, (bank + AHEAD) % BANKS
                if live(later_t):
                    product_pass(later_t, later_bank)
                    square(later_t, later_bank)
                    if later_bank % PRODUCT_BANKS == PRODUCT_BANKS - 1:
                        gate_var(later_t, later_bank // PRODUCT_BANKS)
                if later_bank == BANKS - 1 and (live(t) or live(t - 2)):
                    power(t)
                if bank == 3 and live(t - 1):
                    turn_back(t - 1)
                if t == 0 and bank in (0, 4):
                    mean_passes(1, bank // PRODUCT_BANKS)
                    mean(1, bank // PRODUCT_BANKS)
                if t == 0 and bank in (5, 6):
                    turn(bank - 3)
                    regroup(bank - 3)

            if t == 0:
                quantise(2)
            if live(t + 2):
                mean_passes(t + 2, 0)
            if live(t - 1):
                new_cell(t - 1)
            if live(t + 3):
                quantise(t + 3)
            if live(t):
                scale_ig(t, 0)
                scale_ig(t, 1)
            if live(t + 2):
                mean(t + 2, 0)
            if live(t):
                turned_gate(t, 0)
                turned_gate(t, 2)
            if live(t - 1):
                cell_stats(t - 1)
                squash_o(t - 1)
            if live(t):
                squash_i(t)
                squash_g(t)
                scale_and_shift(t)
            if live(t - 2):
                cell_centre_and_gain(t - 2)
            if live(t + 4):
                turn(t + 4)
                regroup(t + 4)
            if live(t):
                scale_and_add(t)
                squash_f(t)
            if live(t - 2):
                cell_scale_and_shift(t - 2)
                squash_cell(t - 2)
            if live(t + 2):
                mean_passes(t + 2, 1)
                mean(t + 2, 1)
            if live(t - 3) and not live(t):
                hidden(helper, t - 3)
